import numpy as np
import ml_dtypes


def mxq(x, axis, fmt="e4m3"):
    dtype, down = {"e4m3": (ml_dtypes.float8_e4m3fn, 7), "e5m2": (ml_dtypes.float8_e5m2, 14)}[fmt]
    v = np.moveaxis(np.asarray(x, np.float32).astype(ml_dtypes.bfloat16).astype(np.float64), axis, -1)
    blocks = v.reshape(v.shape[:-1] + (-1, 32))
    amax = np.abs(blocks).max(-1, keepdims=True)
    byte = np.maximum(np.where(amax > 0, np.frexp(amax)[1] - 1 + 127, 0) - down, 1)
    scale = np.exp2(byte - 127.0)
    codes = (blocks / scale).astype(np.float32).astype(dtype).astype(np.float64)
    return np.moveaxis((codes * scale).reshape(v.shape), -1, axis)


WIDE = False


def mx_kscale(k):
    if not WIDE:
        return np.ones(k)
    levels = np.array([10, -10, 5, -5, 0])
    a = np.random.permutation(np.resize(levels, k // 512 * 4)).reshape(k // 512, 4)
    idx = np.arange(k)
    return np.exp2(a[idx // 512, idx % 128 // 32])


BF16 = ml_dtypes.bfloat16


def bf(x):
    return np.asarray(x, np.float32).astype(BF16)


def f64(x):
    return np.asarray(x).astype(np.float64)


E2M1 = np.array([0.0, 0.5, 1.0, 1.5, 2.0, 3.0, 4.0, 6.0, -0.0, -0.5, -1.0, -1.5, -2.0, -3.0, -4.0, -6.0])


def pack_weight(w, fmt):
    k, n = w.shape
    w = f64(bf(w)).reshape(k // 32, 32, n)
    amax = np.abs(w).max(1)
    if fmt == "e4m3":
        byte = np.frexp(amax)[1] - 1 + 127 - 7
    else:
        mant, ex = np.frexp(amax / 6.0)
        byte = np.where(mant > 0.5, ex, ex - 1) + 127
    byte = np.clip(np.where(amax > 0, byte, 1), 1, 254)
    scaled = (w * np.exp2(127.0 - byte)[:, None, :]).reshape(k, n).astype(np.float32)
    by_word = np.ascontiguousarray(scaled.reshape(k // 512, 128, 4, n).transpose(0, 1, 3, 2))
    if fmt == "e4m3":
        words = by_word.astype(ml_dtypes.float8_e4m3fn).view(np.uint8)
    else:
        c = by_word.astype(ml_dtypes.float4_e2m1fn).view(np.uint8) & 0xF
        words = c[..., 0::2] | (c[..., 1::2] << 4)
    return np.ascontiguousarray(words), np.ascontiguousarray(byte.astype(np.uint8).reshape(k // 512, 16, n))


def unpack_weight(words, scales, fmt):
    g, p, n, _ = words.shape
    if fmt == "e4m3":
        vals = np.ascontiguousarray(words).view(ml_dtypes.float8_e4m3fn).astype(np.float64)
    else:
        nib = np.empty((g, p, n, 4), np.uint8)
        nib[..., 0::2] = words & 0xF
        nib[..., 1::2] = words >> 4
        vals = E2M1[nib]
    vals = vals * np.repeat(np.exp2(scales.astype(np.float64) - 127.0), 8, axis=1)[..., None]
    return vals.transpose(0, 1, 3, 2).reshape(g * 512, n)


B, H, W, C, D, P = 128, 4, 7, 512, 256, 128
F = H * W * D
STRIDE = 16.0
FMT = "e4m3"


def safe_exp(v):
    return np.exp(np.clip(v, -10.0, 10.0))


def setup_inputs():
    s = mx_kscale(C)
    t = mx_kscale(F)[:D]
    tf = np.tile(t, H * W)[:, None]
    features = bf(np.random.standard_normal((B, H, W, C)) * s)
    roi = bf(np.random.uniform(0.02, 0.125, (B, P, 4)))
    conv_w_words, conv_w_scales = pack_weight(np.random.standard_normal((C, D)) / np.sqrt(C) / s[:, None] * t, FMT)
    conv_b = bf(np.random.standard_normal(D) * 0.2 * t)
    cls_w_words, cls_w_scales = pack_weight(np.random.standard_normal((F, 2 * P)) * 1.5 / np.sqrt(F) / tf, FMT)
    cls_b = bf(np.random.standard_normal(2 * P) * 0.5)
    bbox_w_words, bbox_w_scales = pack_weight(np.random.standard_normal((F, 4 * P)) * 0.7 / np.sqrt(F) / tf, FMT)
    bbox_b = bf(np.random.standard_normal(4 * P) * 0.3)
    return {"features": features,
            "roi": roi,
            "conv_w_words": conv_w_words,
            "conv_w_scales": conv_w_scales,
            "conv_b": conv_b,
            "cls_w_words": cls_w_words,
            "cls_w_scales": cls_w_scales,
            "cls_b": cls_b,
            "bbox_w_words": bbox_w_words,
            "bbox_w_scales": bbox_w_scales,
            "bbox_b": bbox_b}


def reference(features, roi, conv_w_words, conv_w_scales, conv_b, cls_w_words, cls_w_scales, cls_b, bbox_w_words, bbox_w_scales, bbox_b):
    h = np.maximum((mxq(f64(features).reshape(B * H * W, C), 1, "e4m3") @ unpack_weight(conv_w_words, conv_w_scales, FMT)) + f64(conv_b), 0.0)
    flatq = mxq(h.reshape(B, F), 1, "e4m3")
    cls = (flatq @ unpack_weight(cls_w_words, cls_w_scales, FMT)) + f64(cls_b)
    bbox = (flatq @ unpack_weight(bbox_w_words, bbox_w_scales, FMT)[:, P:]) + f64(bbox_b)[P:]
    obj = np.stack([cls[:, :P], cls[:, P:]], axis=0)
    e = np.exp(obj - obj.max(axis=0, keepdims=True))
    objectness = (e / e.sum(axis=0, keepdims=True))[1]
    roi_img = f64(roi) * STRIDE
    bb = np.transpose(bbox.reshape(B, 3, P), (0, 2, 1))
    x = roi_img[:, :, 0] - bb[:, :, 0] * roi_img[:, :, 3]
    y = roi_img[:, :, 1]
    w = roi_img[:, :, 2] * safe_exp(bb[:, :, 1])
    hh = roi_img[:, :, 3] * safe_exp(bb[:, :, 2])
    return np.stack([x, y, w, hh, objectness], axis=-1)

@@ -1,0 +1,309 @@
+from contextlib import ExitStack
+
+import concourse.mybir as mybir
+from concourse.masks import make_identity
+
+F32 = mybir.dt.float32
+BF16 = mybir.dt.bfloat16
+I32 = mybir.dt.int32
+U32 = mybir.dt.uint32
+U8 = mybir.dt.uint8
+FP8X4 = mybir.dt.float8_e4m3fn_x4
+ALU = mybir.AluOpType
+ACT = mybir.ActivationFunctionType
+
+P = 128
+PACK = 4
+POSITIONS = 28
+CHANNELS = 512
+HIDDEN = 256
+PAIRS = POSITIONS // 2
+CLS_COLS = 256
+BOX_SKIP = 128
+BOX_COLS = 384
+HEAD_COLS = CLS_COLS + BOX_COLS
+WIDE = 512
+QUADRANTS = 4
+HEAD_LAG = 10
+
+FLOPS = 2 * P * POSITIONS * CHANNELS * HIDDEN + 2 * P * POSITIONS * HIDDEN * HEAD_COLS
+BYTES = (
+    2 * P * POSITIONS * CHANNELS
+    + 2 * P * P * 4
+    + CHANNELS * HIDDEN + CHANNELS * HIDDEN // 32 + 2 * HIDDEN
+    + POSITIONS * HIDDEN * HEAD_COLS + POSITIONS * HIDDEN * HEAD_COLS // 32 + 2 * HEAD_COLS
+    + 4 * P * P * 5
+)
+
+
+def tile_classifiermodel_kernel(
+    tc,
+    features,
+    roi,
+    conv_w_words,
+    conv_w_scales,
+    conv_b,
+    cls_w_words,
+    cls_w_scales,
+    cls_b,
+    bbox_w_words,
+    bbox_w_scales,
+    bbox_b,
+    out,
+):
+    nc = tc.nc
+    with ExitStack() as stack:
+        keep = stack.enter_context(tc.tile_pool(name="keep", bufs=1))
+        work = stack.enter_context(tc.tile_pool(name="work", bufs=3))
+        psum_x = stack.enter_context(tc.psum_pool(name="psum_x", bufs=2))
+        psum_h = stack.enter_context(tc.psum_pool(name="psum_h", bufs=2))
+        psum_t = stack.enter_context(tc.psum_pool(name="psum_t", bufs=2))
+        psum_acc = stack.enter_context(tc.psum_pool(name="psum_acc", bufs=1))
+        stack.enter_context(tc.manual_schedule())
+
+        x_sb = keep.tile([P, POSITIONS, CHANNELS], BF16)
+        conv_codes = keep.tile([P, HIDDEN], U32, align_bytes=64)
+        conv_plane = keep.tile([P, HIDDEN], U8, align_bytes=64)
+        head_codes = keep.tile([P, PAIRS, HEAD_COLS], U32, align_bytes=64)
+        head_planes = keep.tile([P, PAIRS, HEAD_COLS], U8, align_bytes=64)
+        flat_codes = keep.tile([P, PAIRS, P], U32, align_bytes=64)
+        flat_planes = keep.tile([P, PAIRS, P], U8, align_bytes=64)
+        roi_sb = keep.tile([P, P * 4], BF16)
+        bias_rows = keep.tile([P, HIDDEN + HEAD_COLS + P], BF16)
+        ones = keep.tile([P, P], BF16)
+        ident_f32 = keep.tile([P, P], F32)
+        ident_bf16 = keep.tile([P, P], BF16)
+        conv_bias = keep.tile([P, PACK, P], F32)
+        head_bias = keep.tile([P, HEAD_COLS], F32)
+        table_warm = keep.tile([P, 1], F32)
+
+        nc.vector.memset(conv_plane[:].bitcast(I32), 0)
+        nc.vector.memset(bias_rows[:], 0.0)
+        nc.vector.memset(ones[:], 1.0)
+        nc.vector.memset(head_planes[:].rearrange("p g n -> p (g n)").bitcast(I32), 0)
+        make_identity(nc, ident_f32[:])
+        make_identity(nc, ident_bf16[:])
+
+        x_dram = features.rearrange("b h w c -> b (h w) c")
+
+        def load_features(first_pair, n_pairs):
+            rows = slice(2 * first_pair, 2 * (first_pair + n_pairs))
+            nc.sync.dma_start(out=x_sb[:, rows, :], in_=x_dram[:, rows, :])
+
+        load_features(0, 1)
+        nc.sync.dma_start(
+            out=conv_codes[:].bitcast(I32),
+            in_=conv_w_words[0].rearrange("p n t -> p (n t)").bitcast(I32),
+        )
+        for q in range(QUADRANTS):
+            nc.sync.dma_start(
+                out=conv_plane[32 * q : 32 * q + 4, :].bitcast(I32),
+                in_=conv_w_scales[0, 4 * q : 4 * q + 4, :].bitcast(I32),
+            )
+        load_features(1, 1)
+        for first_pair in range(2, PAIRS, 2):
+            load_features(first_pair, 2)
+        nc.sync.dma_start(out=roi_sb[:], in_=roi.rearrange("b i j -> b (i j)"))
+        nc.sync.dma_start(out=bias_rows[0:1, HIDDEN : HIDDEN + CLS_COLS], in_=cls_b.rearrange("(o d) -> o d", o=1))
+        nc.sync.dma_start(
+            out=bias_rows[0:1, HIDDEN + CLS_COLS : HIDDEN + HEAD_COLS], in_=bbox_b[BOX_SKIP:].rearrange("(o d) -> o d", o=1)
+        )
+        for q in range(QUADRANTS):
+            nc.sync.dma_start(
+                out=head_planes[32 * q : 32 * q + 4, :, 0:CLS_COLS].bitcast(I32),
+                in_=cls_w_scales[:, 4 * q : 4 * q + 4, :].rearrange("g r n -> r g n").bitcast(I32),
+            )
+            nc.sync.dma_start(
+                out=head_planes[32 * q : 32 * q + 4, :, CLS_COLS:HEAD_COLS].bitcast(I32),
+                in_=bbox_w_scales[:, 4 * q : 4 * q + 4, BOX_SKIP:].rearrange("g r n -> r g n").bitcast(I32),
+            )
+        for g in range(0, PAIRS, 2):
+            nc.sync.dma_start(
+                out=head_codes[:, g : g + 2, 0:CLS_COLS].bitcast(I32),
+                in_=cls_w_words[g : g + 2].rearrange("g p n t -> p g (n t)").bitcast(I32),
+            )
+            nc.sync.dma_start(
+                out=head_codes[:, g : g + 2, CLS_COLS:HEAD_COLS].bitcast(I32),
+                in_=bbox_w_words[g : g + 2, :, BOX_SKIP:, :].rearrange("g p n t -> p g (n t)").bitcast(I32),
+            )
+
+        nc.scalar.dma_start(out=bias_rows[0:1, 0:HIDDEN], in_=conv_b.rearrange("(o d) -> o d", o=1))
+        nc.scalar.activation(out=table_warm[:], in_=ones[:, 0:1], func=ACT.Exp)
+
+        x_words = x_sb[:].bitcast(F32)
+        x_t = {}
+        x_grouped = {}
+        x_codes = {}
+        x_planes = {}
+        h_acc = {}
+        h_sorted = {}
+        h_t = {}
+        h_grouped = {}
+
+        def transpose_features(g):
+            x_t[g] = psum_x.tile([P, 2, 2, P], F32, name="x_t")
+            for l in range(2):
+                for u in range(2):
+                    nc.tensor.transpose(
+                        x_t[g][:, l, u, :], x_words[:, 2 * g + l, u : CHANNELS // 2 : 2], ident_f32[:]
+                    )
+
+        def regroup_features(g):
+            x_grouped[g] = work.tile([P, 2, P, PACK], BF16, name="x_grouped", align_bytes=64)
+            nc.scalar.copy(out=x_grouped[g][:].bitcast(F32), in_=x_t[g][:].rearrange("p l u b -> p l b u"))
+
+        def quantise_features(g):
+            x_codes[g] = work.tile([P, 2 * P], U32, name="x_codes", align_bytes=64)
+            x_planes[g] = work.tile([P, 2 * P], U8, name="x_planes", align_bytes=64)
+            nc.vector.quantize_mx(
+                out=x_codes[g][:].bitcast(FP8X4),
+                scales=x_planes[g][:],
+                in_=x_grouped[g][:].rearrange("p l b t -> p (l b t)"),
+            )
+
+        def convolve(g):
+            h_acc[g] = psum_h.tile([P, 2 * HIDDEN], F32, name="h_acc")
+            for l in range(2):
+                nc.tensor.matmul_mx(
+                    out=h_acc[g][:, HIDDEN * l : HIDDEN * (l + 1)],
+                    lhsT=x_codes[g][:, P * l : P * (l + 1)].bitcast(FP8X4),
+                    lhsT_scale=x_planes[g][:, P * l : P * (l + 1)],
+                    rhs=conv_codes[:].bitcast(FP8X4),
+                    rhs_scale=conv_plane[:],
+                    start=True,
+                    stop=True,
+                )
+
+        def add_conv_bias(g):
+            h_sorted[g] = work.tile([P, PACK, P], BF16, name="h_sorted")
+            nc.vector.tensor_tensor(
+                out=h_sorted[g][:],
+                in0=h_acc[g][:].rearrange("b (p t) -> b t p", t=PACK),
+                in1=conv_bias[:],
+                op=ALU.add,
+            )
+
+        def transpose_hidden(g):
+            h_t[g] = psum_t.tile([P, PACK, P], BF16, name="h_t")
+            for t in range(PACK):
+                nc.tensor.transpose(h_t[g][:, t, :], h_sorted[g][:, t, :], ident_bf16[:])
+
+        def relu_and_regroup(g):
+            h_grouped[g] = work.tile([P, P, PACK], BF16, name="h_grouped", align_bytes=64)
+            nc.scalar.activation(out=h_grouped[g][:], in_=h_t[g][:].rearrange("p t b -> p b t"), func=ACT.Relu)
+
+        def quantise_hidden(g):
+            nc.vector.quantize_mx(
+                out=flat_codes[:, g, :].bitcast(FP8X4),
+                scales=flat_planes[:, g, :],
+                in_=h_grouped[g][:].rearrange("p b t -> p (b t)"),
+            )
+
+        acc_wide = psum_acc.tile([P, WIDE], F32)
+        acc_rest = psum_acc.tile([P, HEAD_COLS - WIDE], F32)
+
+        def heads(g):
+            for acc, cols in ((acc_wide, slice(0, WIDE)), (acc_rest, slice(WIDE, HEAD_COLS))):
+                nc.tensor.matmul_mx(
+                    out=acc[:],
+                    lhsT=flat_codes[:, g, :].bitcast(FP8X4),
+                    lhsT_scale=flat_planes[:, g, :],
+                    rhs=head_codes[:, g, cols].bitcast(FP8X4),
+                    rhs_scale=head_planes[:, g, cols],
+                    start=(g == 0),
+                    stop=(g == PAIRS - 1),
+                )
+
+        def spread_conv_bias():
+            spread = psum_h.tile([P, 2 * HIDDEN], F32, name="h_acc")
+            nc.tensor.matmul(out=spread[:, 0:HIDDEN], lhsT=ones[:], rhs=bias_rows[:, 0:HIDDEN], start=True, stop=True)
+            nc.vector.tensor_copy(
+                out=conv_bias[:].rearrange("b t (l j) -> b t l j", l=2),
+                in_=spread[:, 0:HIDDEN]
+                .rearrange("b (j t) -> b t j", t=PACK)
+                .unsqueeze(2)
+                .to_broadcast([P, PACK, 2, HIDDEN // PACK]),
+            )
+
+        def spread_head_bias():
+            spread_wide = psum_x.tile([P, WIDE], F32, name="x_t")
+            nc.tensor.matmul(
+                out=spread_wide[:], lhsT=ones[:], rhs=bias_rows[:, HIDDEN : HIDDEN + WIDE], start=True, stop=True
+            )
+            nc.vector.tensor_copy(out=head_bias[:, 0:WIDE], in_=spread_wide[:])
+            spread_rest = psum_x.tile([P, WIDE], F32, name="x_t")
+            nc.tensor.matmul(
+                out=spread_rest[:, 0 : 2 * P],
+                lhsT=ones[:],
+                rhs=bias_rows[:, HIDDEN + WIDE : HIDDEN + WIDE + 2 * P],
+                start=True,
+                stop=True,
+            )
+            nc.vector.tensor_copy(out=head_bias[:, WIDE:HEAD_COLS], in_=spread_rest[:, 0 : HEAD_COLS - WIDE])
+
+        def live(g):
+            return 0 <= g < PAIRS
+
+        def pipeline_step(step):
+            if live(step):
+                transpose_features(step)
+            if live(step - 4):
+                transpose_hidden(step - 4)
+            if live(step):
+                regroup_features(step)
+            if live(step - 4):
+                relu_and_regroup(step - 4)
+            if live(step - 1):
+                quantise_features(step - 1)
+            if live(step - 5):
+                quantise_hidden(step - 5)
+            if live(step - 2):
+                convolve(step - 2)
+            if live(step - HEAD_LAG):
+                heads(step - HEAD_LAG)
+            if live(step - 2):
+                add_conv_bias(step - 2)
+
+        spread_conv_bias()
+        for step in range(PAIRS):
+            pipeline_step(step)
+        spread_head_bias()
+        for step in range(PAIRS, PAIRS + HEAD_LAG):
+            pipeline_step(step)
+
+        planes = keep.tile([P, 5, P], F32)
+        r = keep.tile([P, 4, P], F32)
+        nc.gpsimd.tensor_scalar(
+            out=r[:], in0=roi_sb[:].rearrange("b (i j) -> b j i", j=4), scalar1=16.0, scalar2=0.0, op0=ALU.mult, op1=ALU.add
+        )
+        nc.gpsimd.tensor_scalar(out=planes[:, 1, :], in0=r[:, 1, :], scalar1=1.0, scalar2=0.0, op0=ALU.mult, op1=ALU.add)
+
+        z = keep.tile([P, 5, P], F32)
+        z_flat = z[:].rearrange("b j i -> b (j i)")
+        top = keep.tile([P, P], F32)
+        logits = keep.tile([P, 2, P], F32)
+        clipped = keep.tile([P, 2, P], F32)
+        e_logits = keep.tile([P, 2, P], F32)
+        e_clipped = keep.tile([P, 2, P], F32)
+        shift = keep.tile([P, P], F32)
+        total = keep.tile([P, P], F32)
+        result = keep.tile([P, P, 5], F32)
+        half = WIDE // 2
+        nc.vector.tensor_tensor(out=z_flat[:, 0:half], in0=acc_wide[:, 0:half], in1=head_bias[:, 0:half], op=ALU.add)
+        nc.vector.tensor_tensor(out=z_flat[:, half:WIDE], in0=acc_wide[:, half:WIDE], in1=head_bias[:, half:WIDE], op=ALU.add)
+        nc.vector.tensor_tensor(out=top[:], in0=z[:, 0, :], in1=z[:, 1, :], op=ALU.max)
+        nc.vector.tensor_tensor(out=z_flat[:, WIDE:HEAD_COLS], in0=acc_rest[:], in1=head_bias[:, WIDE:HEAD_COLS], op=ALU.add)
+        nc.vector.tensor_tensor(
+            out=logits[:], in0=z[:, 0:2, :], in1=top[:].unsqueeze(1).to_broadcast([P, 2, P]), op=ALU.subtract
+        )
+        nc.scalar.activation(out=e_logits[:], in_=logits[:], func=ACT.Exp)
+        nc.vector.tensor_scalar(out=clipped[:], in0=z[:, 3:5, :], scalar1=-10.0, scalar2=10.0, op0=ALU.max, op1=ALU.min)
+        nc.scalar.activation(out=e_clipped[:], in_=clipped[:], func=ACT.Exp)
+        nc.vector.tensor_tensor(out=shift[:], in0=z[:, 2, :], in1=r[:, 3, :], op=ALU.mult)
+        nc.vector.tensor_tensor(out=planes[:, 0, :], in0=r[:, 0, :], in1=shift[:], op=ALU.subtract)
+        nc.vector.tensor_tensor(out=total[:], in0=e_logits[:, 0, :], in1=e_logits[:, 1, :], op=ALU.add)
+        nc.vector.tensor_tensor(out=planes[:, 2:4, :], in0=r[:, 2:4, :], in1=e_clipped[:], op=ALU.mult)
+        nc.vector.reciprocal(out=total[:], in_=total[:])
+        nc.vector.tensor_tensor(out=planes[:, 4, :], in0=e_logits[:, 1, :], in1=total[:], op=ALU.mult)
+        nc.vector.tensor_copy(out=result[:], in_=planes[:].rearrange("b j i -> b i j"))
+        nc.sync.dma_start(out=out.rearrange("b i j -> b (i j)"), in_=result[:].rearrange("b i j -> b (i j)"))

@@ -77,12 +77,10 @@ def tile_classifiermodel_kernel(
         head_bias = keep.tile([P, HEAD_COLS], F32)
         table_warm = keep.tile([P, 1], F32)
 
-        nc.vector.memset(conv_plane[:].bitcast(I32), 0)
         nc.vector.memset(bias_rows[:], 0.0)
-        nc.vector.memset(ones[:], 1.0)
+        nc.vector.memset(conv_plane[:].bitcast(I32), 0)
         nc.vector.memset(head_planes[:].rearrange("p g n -> p (g n)").bitcast(I32), 0)
-        make_identity(nc, ident_f32[:])
-        make_identity(nc, ident_bf16[:])
+        nc.vector.memset(ones[:], 1.0)
 
         x_dram = features.rearrange("b h w c -> b (h w) c")
 
@@ -95,28 +93,15 @@ def tile_classifiermodel_kernel(
             out=conv_codes[:].bitcast(I32),
             in_=conv_w_words[0].rearrange("p n t -> p (n t)").bitcast(I32),
         )
+        load_features(1, 1)
+        load_features(2, 4)
         for q in range(QUADRANTS):
             nc.sync.dma_start(
                 out=conv_plane[32 * q : 32 * q + 4, :].bitcast(I32),
                 in_=conv_w_scales[0, 4 * q : 4 * q + 4, :].bitcast(I32),
             )
-        load_features(1, 1)
-        for first_pair in range(2, PAIRS, 2):
-            load_features(first_pair, 2)
-        nc.sync.dma_start(out=roi_sb[:], in_=roi.rearrange("b i j -> b (i j)"))
-        nc.sync.dma_start(out=bias_rows[0:1, HIDDEN : HIDDEN + CLS_COLS], in_=cls_b.rearrange("(o d) -> o d", o=1))
-        nc.sync.dma_start(
-            out=bias_rows[0:1, HIDDEN + CLS_COLS : HIDDEN + HEAD_COLS], in_=bbox_b[BOX_SKIP:].rearrange("(o d) -> o d", o=1)
-        )
-        for q in range(QUADRANTS):
-            nc.sync.dma_start(
-                out=head_planes[32 * q : 32 * q + 4, :, 0:CLS_COLS].bitcast(I32),
-                in_=cls_w_scales[:, 4 * q : 4 * q + 4, :].rearrange("g r n -> r g n").bitcast(I32),
-            )
-            nc.sync.dma_start(
-                out=head_planes[32 * q : 32 * q + 4, :, CLS_COLS:HEAD_COLS].bitcast(I32),
-                in_=bbox_w_scales[:, 4 * q : 4 * q + 4, BOX_SKIP:].rearrange("g r n -> r g n").bitcast(I32),
-            )
+        load_features(6, 4)
+        load_features(10, 4)
         for g in range(0, PAIRS, 2):
             nc.sync.dma_start(
                 out=head_codes[:, g : g + 2, 0:CLS_COLS].bitcast(I32),
@@ -127,7 +112,24 @@ def tile_classifiermodel_kernel(
                 in_=bbox_w_words[g : g + 2, :, BOX_SKIP:, :].rearrange("g p n t -> p g (n t)").bitcast(I32),
             )
 
-        nc.scalar.dma_start(out=bias_rows[0:1, 0:HIDDEN], in_=conv_b.rearrange("(o d) -> o d", o=1))
+        nc.gpsimd.dma_start(out=bias_rows[0:1, 0:HIDDEN], in_=conv_b.rearrange("(o d) -> o d", o=1))
+        make_identity(nc, ident_f32[:])
+        for q in range(QUADRANTS):
+            nc.gpsimd.dma_start(
+                out=head_planes[32 * q : 32 * q + 4, :, 0:CLS_COLS].bitcast(F32),
+                in_=cls_w_scales[:, 4 * q : 4 * q + 4, :].rearrange("g r n -> r g n").bitcast(F32),
+            )
+            nc.gpsimd.dma_start(
+                out=head_planes[32 * q : 32 * q + 4, :, CLS_COLS:HEAD_COLS].bitcast(F32),
+                in_=bbox_w_scales[:, 4 * q : 4 * q + 4, BOX_SKIP:].rearrange("g r n -> r g n").bitcast(F32),
+            )
+        nc.gpsimd.dma_start(out=bias_rows[0:1, HIDDEN : HIDDEN + CLS_COLS], in_=cls_b.rearrange("(o d) -> o d", o=1))
+        nc.gpsimd.dma_start(
+            out=bias_rows[0:1, HIDDEN + CLS_COLS : HIDDEN + HEAD_COLS], in_=bbox_b[BOX_SKIP:].rearrange("(o d) -> o d", o=1)
+        )
+        nc.gpsimd.dma_start(out=roi_sb[:], in_=roi.rearrange("b i j -> b (i j)"))
+
+        nc.vector.tensor_copy(out=ident_bf16[:], in_=ident_f32[:])
         nc.scalar.activation(out=table_warm[:], in_=ones[:, 0:1], func=ACT.Exp)
 
         x_words = x_sb[:].bitcast(F32)

@@ -24,6 +24,7 @@ BOX_COLS = 384
 HEAD_COLS = CLS_COLS + BOX_COLS
 WIDE = 512
 QUADRANTS = 4
+WARM_MATMULS = 6
 HEAD_LAG = 10
 
 FLOPS = 2 * P * POSITIONS * CHANNELS * HIDDEN + 2 * P * POSITIONS * HIDDEN * HEAD_COLS
@@ -76,11 +77,13 @@ def tile_classifiermodel_kernel(
         conv_bias = keep.tile([P, PACK, P], F32)
         head_bias = keep.tile([P, HEAD_COLS], F32)
         table_warm = keep.tile([P, 1], F32)
+        zeros = keep.tile([P, WIDE], BF16)
 
+        nc.vector.memset(zeros[:], 0.0)
+        nc.vector.memset(ones[:], 1.0)
         nc.vector.memset(bias_rows[:], 0.0)
         nc.vector.memset(conv_plane[:].bitcast(I32), 0)
         nc.vector.memset(head_planes[:].rearrange("p g n -> p (g n)").bitcast(I32), 0)
-        nc.vector.memset(ones[:], 1.0)
 
         x_dram = features.rearrange("b h w c -> b (h w) c")
 
@@ -112,7 +115,6 @@ def tile_classifiermodel_kernel(
                 in_=bbox_w_words[g : g + 2, :, BOX_SKIP:, :].rearrange("g p n t -> p g (n t)").bitcast(I32),
             )
 
-        nc.gpsimd.dma_start(out=bias_rows[0:1, 0:HIDDEN], in_=conv_b.rearrange("(o d) -> o d", o=1))
         make_identity(nc, ident_f32[:])
         for q in range(QUADRANTS):
             nc.gpsimd.dma_start(
@@ -130,6 +132,7 @@ def tile_classifiermodel_kernel(
         nc.gpsimd.dma_start(out=roi_sb[:], in_=roi.rearrange("b i j -> b (i j)"))
 
         nc.vector.tensor_copy(out=ident_bf16[:], in_=ident_f32[:])
+        nc.scalar.dma_start(out=bias_rows[0:1, 0:HIDDEN], in_=conv_b.rearrange("(o d) -> o d", o=1))
         nc.scalar.activation(out=table_warm[:], in_=ones[:, 0:1], func=ACT.Exp)
 
         x_words = x_sb[:].bitcast(F32)
@@ -216,6 +219,21 @@ def tile_classifiermodel_kernel(
                     stop=(g == PAIRS - 1),
                 )
 
+        def warm_clock():
+            nc.tensor.matmul(out=acc_wide[:], lhsT=ones[:], rhs=zeros[:], start=True, stop=True)
+
+        def keep_clock():
+            for repeat in range(2):
+                nc.tensor.matmul_mx(
+                    out=acc_wide[:, 0:HIDDEN],
+                    lhsT=conv_codes[:, 0:P].bitcast(FP8X4),
+                    lhsT_scale=conv_plane[:, 0:P],
+                    rhs=conv_codes[:].bitcast(FP8X4),
+                    rhs_scale=conv_plane[:],
+                    start=True,
+                    stop=True,
+                )
+
         def spread_conv_bias():
             spread = psum_h.tile([P, 2 * HIDDEN], F32, name="h_acc")
             nc.tensor.matmul(out=spread[:, 0:HIDDEN], lhsT=ones[:], rhs=bias_rows[:, 0:HIDDEN], start=True, stop=True)
@@ -263,9 +281,13 @@ def tile_classifiermodel_kernel(
                 convolve(step - 2)
             if live(step - HEAD_LAG):
                 heads(step - HEAD_LAG)
+            if step < HEAD_LAG:
+                keep_clock()
             if live(step - 2):
                 add_conv_bias(step - 2)
 
+        for warm in range(WARM_MATMULS):
+            warm_clock()
         spread_conv_bias()
         for step in range(PAIRS):
             pipeline_step(step)

@@ -21,10 +21,9 @@ PAIRS = POSITIONS // 2
 CLS_COLS = 256
 BOX_SKIP = 128
 BOX_COLS = 384
-HEAD_COLS = CLS_COLS + BOX_COLS
+HEAD_COLS = BOX_COLS + CLS_COLS
 WIDE = 512
 QUADRANTS = 4
-WARM_MATMULS = 6
 HEAD_LAG = 10
 
 FLOPS = 2 * P * POSITIONS * CHANNELS * HIDDEN + 2 * P * POSITIONS * HIDDEN * HEAD_COLS
@@ -77,13 +76,11 @@ def tile_classifiermodel_kernel(
         conv_bias = keep.tile([P, PACK, P], F32)
         head_bias = keep.tile([P, HEAD_COLS], F32)
         table_warm = keep.tile([P, 1], F32)
-        zeros = keep.tile([P, WIDE], BF16)
 
-        nc.vector.memset(zeros[:], 0.0)
-        nc.vector.memset(ones[:], 1.0)
         nc.vector.memset(bias_rows[:], 0.0)
         nc.vector.memset(conv_plane[:].bitcast(I32), 0)
         nc.vector.memset(head_planes[:].rearrange("p g n -> p (g n)").bitcast(I32), 0)
+        nc.vector.memset(ones[:], 1.0)
 
         x_dram = features.rearrange("b h w c -> b (h w) c")
 
@@ -96,38 +93,39 @@ def tile_classifiermodel_kernel(
             out=conv_codes[:].bitcast(I32),
             in_=conv_w_words[0].rearrange("p n t -> p (n t)").bitcast(I32),
         )
-        load_features(1, 1)
-        load_features(2, 4)
         for q in range(QUADRANTS):
             nc.sync.dma_start(
                 out=conv_plane[32 * q : 32 * q + 4, :].bitcast(I32),
                 in_=conv_w_scales[0, 4 * q : 4 * q + 4, :].bitcast(I32),
             )
+        load_features(1, 1)
+        load_features(2, 2)
+        load_features(4, 2)
         load_features(6, 4)
         load_features(10, 4)
         for g in range(0, PAIRS, 2):
             nc.sync.dma_start(
-                out=head_codes[:, g : g + 2, 0:CLS_COLS].bitcast(I32),
+                out=head_codes[:, g : g + 2, BOX_COLS:HEAD_COLS].bitcast(I32),
                 in_=cls_w_words[g : g + 2].rearrange("g p n t -> p g (n t)").bitcast(I32),
             )
             nc.sync.dma_start(
-                out=head_codes[:, g : g + 2, CLS_COLS:HEAD_COLS].bitcast(I32),
+                out=head_codes[:, g : g + 2, 0:BOX_COLS].bitcast(I32),
                 in_=bbox_w_words[g : g + 2, :, BOX_SKIP:, :].rearrange("g p n t -> p g (n t)").bitcast(I32),
             )
 
         make_identity(nc, ident_f32[:])
         for q in range(QUADRANTS):
             nc.gpsimd.dma_start(
-                out=head_planes[32 * q : 32 * q + 4, :, 0:CLS_COLS].bitcast(F32),
+                out=head_planes[32 * q : 32 * q + 4, :, BOX_COLS:HEAD_COLS].bitcast(F32),
                 in_=cls_w_scales[:, 4 * q : 4 * q + 4, :].rearrange("g r n -> r g n").bitcast(F32),
             )
             nc.gpsimd.dma_start(
-                out=head_planes[32 * q : 32 * q + 4, :, CLS_COLS:HEAD_COLS].bitcast(F32),
+                out=head_planes[32 * q : 32 * q + 4, :, 0:BOX_COLS].bitcast(F32),
                 in_=bbox_w_scales[:, 4 * q : 4 * q + 4, BOX_SKIP:].rearrange("g r n -> r g n").bitcast(F32),
             )
-        nc.gpsimd.dma_start(out=bias_rows[0:1, HIDDEN : HIDDEN + CLS_COLS], in_=cls_b.rearrange("(o d) -> o d", o=1))
+        nc.gpsimd.dma_start(out=bias_rows[0:1, HIDDEN + BOX_COLS : HIDDEN + HEAD_COLS], in_=cls_b.rearrange("(o d) -> o d", o=1))
         nc.gpsimd.dma_start(
-            out=bias_rows[0:1, HIDDEN + CLS_COLS : HIDDEN + HEAD_COLS], in_=bbox_b[BOX_SKIP:].rearrange("(o d) -> o d", o=1)
+            out=bias_rows[0:1, HIDDEN : HIDDEN + BOX_COLS], in_=bbox_b[BOX_SKIP:].rearrange("(o d) -> o d", o=1)
         )
         nc.gpsimd.dma_start(out=roi_sb[:], in_=roi.rearrange("b i j -> b (i j)"))
 
@@ -204,11 +202,11 @@ def tile_classifiermodel_kernel(
                 in_=h_grouped[g][:].rearrange("p b t -> p (b t)"),
             )
 
+        acc_b1 = psum_acc.tile([P, P], F32)
         acc_wide = psum_acc.tile([P, WIDE], F32)
-        acc_rest = psum_acc.tile([P, HEAD_COLS - WIDE], F32)
 
         def heads(g):
-            for acc, cols in ((acc_wide, slice(0, WIDE)), (acc_rest, slice(WIDE, HEAD_COLS))):
+            for acc, cols in ((acc_b1, slice(0, P)), (acc_wide, slice(P, HEAD_COLS))):
                 nc.tensor.matmul_mx(
                     out=acc[:],
                     lhsT=flat_codes[:, g, :].bitcast(FP8X4),
@@ -217,21 +215,6 @@ def tile_classifiermodel_kernel(
                     rhs_scale=head_planes[:, g, cols],
                     start=(g == 0),
                     stop=(g == PAIRS - 1),
-                )
-
-        def warm_clock():
-            nc.tensor.matmul(out=acc_wide[:], lhsT=ones[:], rhs=zeros[:], start=True, stop=True)
-
-        def keep_clock():
-            for repeat in range(2):
-                nc.tensor.matmul_mx(
-                    out=acc_wide[:, 0:HIDDEN],
-                    lhsT=conv_codes[:, 0:P].bitcast(FP8X4),
-                    lhsT_scale=conv_plane[:, 0:P],
-                    rhs=conv_codes[:].bitcast(FP8X4),
-                    rhs_scale=conv_plane[:],
-                    start=True,
-                    stop=True,
                 )
 
         def spread_conv_bias():
@@ -281,13 +264,9 @@ def tile_classifiermodel_kernel(
                 convolve(step - 2)
             if live(step - HEAD_LAG):
                 heads(step - HEAD_LAG)
-            if step < HEAD_LAG:
-                keep_clock()
             if live(step - 2):
                 add_conv_bias(step - 2)
 
-        for warm in range(WARM_MATMULS):
-            warm_clock()
         spread_conv_bias()
         for step in range(PAIRS):
             pipeline_step(step)
@@ -297,37 +276,35 @@ def tile_classifiermodel_kernel(
 
         planes = keep.tile([P, 5, P], F32)
         r = keep.tile([P, 4, P], F32)
+        x_base = keep.tile([P, P], F32)
         nc.gpsimd.tensor_scalar(
             out=r[:], in0=roi_sb[:].rearrange("b (i j) -> b j i", j=4), scalar1=16.0, scalar2=0.0, op0=ALU.mult, op1=ALU.add
         )
         nc.gpsimd.tensor_scalar(out=planes[:, 1, :], in0=r[:, 1, :], scalar1=1.0, scalar2=0.0, op0=ALU.mult, op1=ALU.add)
+        nc.gpsimd.tensor_tensor(out=x_base[:], in0=head_bias[:, 0:P], in1=r[:, 3, :], op=ALU.mult)
+        nc.gpsimd.tensor_tensor(out=x_base[:], in0=r[:, 0, :], in1=x_base[:], op=ALU.subtract)
 
-        z = keep.tile([P, 5, P], F32)
-        z_flat = z[:].rearrange("b j i -> b (j i)")
-        top = keep.tile([P, P], F32)
+        box = keep.tile([P, 2, P], F32)
         logits = keep.tile([P, 2, P], F32)
-        clipped = keep.tile([P, 2, P], F32)
-        e_logits = keep.tile([P, 2, P], F32)
-        e_clipped = keep.tile([P, 2, P], F32)
+        margin = keep.tile([P, P], F32)
+        tanh_half = keep.tile([P, P], F32)
+        growth = keep.tile([P, 2, P], F32)
         shift = keep.tile([P, P], F32)
-        total = keep.tile([P, P], F32)
         result = keep.tile([P, P, 5], F32)
         half = WIDE // 2
-        nc.vector.tensor_tensor(out=z_flat[:, 0:half], in0=acc_wide[:, 0:half], in1=head_bias[:, 0:half], op=ALU.add)
-        nc.vector.tensor_tensor(out=z_flat[:, half:WIDE], in0=acc_wide[:, half:WIDE], in1=head_bias[:, half:WIDE], op=ALU.add)
-        nc.vector.tensor_tensor(out=top[:], in0=z[:, 0, :], in1=z[:, 1, :], op=ALU.max)
-        nc.vector.tensor_tensor(out=z_flat[:, WIDE:HEAD_COLS], in0=acc_rest[:], in1=head_bias[:, WIDE:HEAD_COLS], op=ALU.add)
         nc.vector.tensor_tensor(
-            out=logits[:], in0=z[:, 0:2, :], in1=top[:].unsqueeze(1).to_broadcast([P, 2, P]), op=ALU.subtract
+            out=logits[:].rearrange("b j i -> b (j i)"), in0=acc_wide[:, half:WIDE], in1=head_bias[:, P + half : HEAD_COLS], op=ALU.add
         )
-        nc.scalar.activation(out=e_logits[:], in_=logits[:], func=ACT.Exp)
-        nc.vector.tensor_scalar(out=clipped[:], in0=z[:, 3:5, :], scalar1=-10.0, scalar2=10.0, op0=ALU.max, op1=ALU.min)
-        nc.scalar.activation(out=e_clipped[:], in_=clipped[:], func=ACT.Exp)
-        nc.vector.tensor_tensor(out=shift[:], in0=z[:, 2, :], in1=r[:, 3, :], op=ALU.mult)
-        nc.vector.tensor_tensor(out=planes[:, 0, :], in0=r[:, 0, :], in1=shift[:], op=ALU.subtract)
-        nc.vector.tensor_tensor(out=total[:], in0=e_logits[:, 0, :], in1=e_logits[:, 1, :], op=ALU.add)
-        nc.vector.tensor_tensor(out=planes[:, 2:4, :], in0=r[:, 2:4, :], in1=e_clipped[:], op=ALU.mult)
-        nc.vector.reciprocal(out=total[:], in_=total[:])
-        nc.vector.tensor_tensor(out=planes[:, 4, :], in0=e_logits[:, 1, :], in1=total[:], op=ALU.mult)
+        nc.vector.tensor_tensor(
+            out=box[:].rearrange("b j i -> b (j i)"), in0=acc_wide[:, 0:half], in1=head_bias[:, P : P + half], op=ALU.add
+        )
+        nc.vector.tensor_tensor(out=margin[:], in0=logits[:, 1, :], in1=logits[:, 0, :], op=ALU.subtract)
+        nc.scalar.activation(out=tanh_half[:], in_=margin[:], func=ACT.Tanh, scale=0.5)
+        nc.vector.tensor_scalar(out=box[:], in0=box[:], scalar1=-10.0, scalar2=10.0, op0=ALU.max, op1=ALU.min)
+        nc.scalar.activation(out=growth[:], in_=box[:], func=ACT.Exp)
+        nc.vector.tensor_tensor(out=shift[:], in0=acc_b1[:], in1=r[:, 3, :], op=ALU.mult)
+        nc.vector.tensor_tensor(out=planes[:, 0, :], in0=x_base[:], in1=shift[:], op=ALU.subtract)
+        nc.vector.tensor_scalar(out=planes[:, 4, :], in0=tanh_half[:], scalar1=0.5, scalar2=0.5, op0=ALU.mult, op1=ALU.add)
+        nc.vector.tensor_tensor(out=planes[:, 2:4, :], in0=r[:, 2:4, :], in1=growth[:], op=ALU.mult)
         nc.vector.tensor_copy(out=result[:], in_=planes[:].rearrange("b j i -> b i j"))
         nc.sync.dma_start(out=out.rearrange("b i j -> b (i j)"), in_=result[:].rearrange("b i j -> b (i j)"))

@@ -24,7 +24,8 @@ BOX_COLS = 384
 HEAD_COLS = BOX_COLS + CLS_COLS
 WIDE = 512
 QUADRANTS = 4
-HEAD_LAG = 10
+HEAD_LAG = 7
+FEATURE_LEAD = 8
 
 FLOPS = 2 * P * POSITIONS * CHANNELS * HIDDEN + 2 * P * POSITIONS * HIDDEN * HEAD_COLS
 BYTES = (
@@ -99,10 +100,17 @@ def tile_classifiermodel_kernel(
                 in_=conv_w_scales[0, 4 * q : 4 * q + 4, :].bitcast(I32),
             )
         load_features(1, 1)
-        load_features(2, 2)
-        load_features(4, 2)
-        load_features(6, 4)
-        load_features(10, 4)
+        for first_pair in range(2, FEATURE_LEAD, 2):
+            load_features(first_pair, 2)
+        for q in range(QUADRANTS):
+            nc.sync.dma_start(
+                out=head_planes[32 * q : 32 * q + 4, :, BOX_COLS:HEAD_COLS].bitcast(I32),
+                in_=cls_w_scales[:, 4 * q : 4 * q + 4, :].rearrange("g r n -> r g n").bitcast(I32),
+            )
+            nc.sync.dma_start(
+                out=head_planes[32 * q : 32 * q + 4, :, 0:BOX_COLS].bitcast(I32),
+                in_=bbox_w_scales[:, 4 * q : 4 * q + 4, BOX_SKIP:].rearrange("g r n -> r g n").bitcast(I32),
+            )
         for g in range(0, PAIRS, 2):
             nc.sync.dma_start(
                 out=head_codes[:, g : g + 2, BOX_COLS:HEAD_COLS].bitcast(I32),
@@ -112,17 +120,10 @@ def tile_classifiermodel_kernel(
                 out=head_codes[:, g : g + 2, 0:BOX_COLS].bitcast(I32),
                 in_=bbox_w_words[g : g + 2, :, BOX_SKIP:, :].rearrange("g p n t -> p g (n t)").bitcast(I32),
             )
+            if FEATURE_LEAD + g < PAIRS:
+                load_features(FEATURE_LEAD + g, 2)
 
         make_identity(nc, ident_f32[:])
-        for q in range(QUADRANTS):
-            nc.gpsimd.dma_start(
-                out=head_planes[32 * q : 32 * q + 4, :, BOX_COLS:HEAD_COLS].bitcast(F32),
-                in_=cls_w_scales[:, 4 * q : 4 * q + 4, :].rearrange("g r n -> r g n").bitcast(F32),
-            )
-            nc.gpsimd.dma_start(
-                out=head_planes[32 * q : 32 * q + 4, :, 0:BOX_COLS].bitcast(F32),
-                in_=bbox_w_scales[:, 4 * q : 4 * q + 4, BOX_SKIP:].rearrange("g r n -> r g n").bitcast(F32),
-            )
         nc.gpsimd.dma_start(out=bias_rows[0:1, HIDDEN + BOX_COLS : HIDDEN + HEAD_COLS], in_=cls_b.rearrange("(o d) -> o d", o=1))
         nc.gpsimd.dma_start(
             out=bias_rows[0:1, HIDDEN : HIDDEN + BOX_COLS], in_=bbox_b[BOX_SKIP:].rearrange("(o d) -> o d", o=1)

@@ -17,15 +17,16 @@ PACK = 4
 POSITIONS = 28
 CHANNELS = 512
 HIDDEN = 256
+LIVE = HIDDEN // PACK
 PAIRS = POSITIONS // 2
+ROUNDS = PAIRS // 2
 CLS_COLS = 256
 BOX_SKIP = 128
 BOX_COLS = 384
 HEAD_COLS = BOX_COLS + CLS_COLS
 WIDE = 512
 QUADRANTS = 4
-HEAD_LAG = 7
-FEATURE_LEAD = 8
+FEATURE_LEAD = 3
 
 FLOPS = 2 * P * POSITIONS * CHANNELS * HIDDEN + 2 * P * POSITIONS * HIDDEN * HEAD_COLS
 BYTES = (
@@ -56,40 +57,42 @@ def tile_classifiermodel_kernel(
     with ExitStack() as stack:
         keep = stack.enter_context(tc.tile_pool(name="keep", bufs=1))
         work = stack.enter_context(tc.tile_pool(name="work", bufs=3))
-        psum_x = stack.enter_context(tc.psum_pool(name="psum_x", bufs=2))
+        psum_x = stack.enter_context(tc.psum_pool(name="psum_x", bufs=4))
         psum_h = stack.enter_context(tc.psum_pool(name="psum_h", bufs=2))
-        psum_t = stack.enter_context(tc.psum_pool(name="psum_t", bufs=2))
         psum_acc = stack.enter_context(tc.psum_pool(name="psum_acc", bufs=1))
         stack.enter_context(tc.manual_schedule())
 
         x_sb = keep.tile([P, POSITIONS, CHANNELS], BF16)
         conv_codes = keep.tile([P, HIDDEN], U32, align_bytes=64)
         conv_plane = keep.tile([P, HIDDEN], U8, align_bytes=64)
+        padded_codes = keep.tile([P, PACK, 3 * LIVE], U32, align_bytes=64)
+        padded_plane = keep.tile([P, PACK, 3 * LIVE], U8, align_bytes=64)
         head_codes = keep.tile([P, PAIRS, HEAD_COLS], U32, align_bytes=64)
         head_planes = keep.tile([P, PAIRS, HEAD_COLS], U8, align_bytes=64)
         flat_codes = keep.tile([P, PAIRS, P], U32, align_bytes=64)
         flat_planes = keep.tile([P, PAIRS, P], U8, align_bytes=64)
         roi_sb = keep.tile([P, P * 4], BF16)
-        bias_rows = keep.tile([P, HIDDEN + HEAD_COLS + P], BF16)
+        bias_rows = keep.tile([P, HEAD_COLS], BF16)
+        conv_bias = keep.tile([P, PACK], BF16)
         ones = keep.tile([P, P], BF16)
         ident_f32 = keep.tile([P, P], F32)
-        ident_bf16 = keep.tile([P, P], BF16)
-        conv_bias = keep.tile([P, PACK, P], F32)
         head_bias = keep.tile([P, HEAD_COLS], F32)
         table_warm = keep.tile([P, 1], F32)
 
-        nc.vector.memset(bias_rows[:], 0.0)
         nc.vector.memset(conv_plane[:].bitcast(I32), 0)
-        nc.vector.memset(head_planes[:].rearrange("p g n -> p (g n)").bitcast(I32), 0)
+        nc.vector.memset(bias_rows[:], 0.0)
         nc.vector.memset(ones[:], 1.0)
+        nc.vector.memset(padded_codes[:].rearrange("p t n -> p (t n)").bitcast(I32), 0)
+        nc.vector.memset(padded_plane[:].rearrange("p t n -> p (t n)").bitcast(I32), 0)
+        nc.vector.memset(head_planes[:].rearrange("p g n -> p (g n)").bitcast(I32), 0)
 
         x_dram = features.rearrange("b h w c -> b (h w) c")
 
-        def load_features(first_pair, n_pairs):
-            rows = slice(2 * first_pair, 2 * (first_pair + n_pairs))
-            nc.sync.dma_start(out=x_sb[:, rows, :], in_=x_dram[:, rows, :])
+        def load_features(r):
+            nc.sync.dma_start(out=x_sb[:, 4 * r : 4 * r + 4, :], in_=x_dram[:, 4 * r : 4 * r + 4, :])
 
-        load_features(0, 1)
+        for l in range(2):
+            nc.sync.dma_start(out=x_sb[:, l:4:2, :], in_=x_dram[:, l:4:2, :])
         nc.sync.dma_start(
             out=conv_codes[:].bitcast(I32),
             in_=conv_w_words[0].rearrange("p n t -> p (n t)").bitcast(I32),
@@ -99,9 +102,8 @@ def tile_classifiermodel_kernel(
                 out=conv_plane[32 * q : 32 * q + 4, :].bitcast(I32),
                 in_=conv_w_scales[0, 4 * q : 4 * q + 4, :].bitcast(I32),
             )
-        load_features(1, 1)
-        for first_pair in range(2, FEATURE_LEAD, 2):
-            load_features(first_pair, 2)
+        for r in range(1, FEATURE_LEAD):
+            load_features(r)
         for q in range(QUADRANTS):
             nc.sync.dma_start(
                 out=head_planes[32 * q : 32 * q + 4, :, BOX_COLS:HEAD_COLS].bitcast(I32),
@@ -111,27 +113,27 @@ def tile_classifiermodel_kernel(
                 out=head_planes[32 * q : 32 * q + 4, :, 0:BOX_COLS].bitcast(I32),
                 in_=bbox_w_scales[:, 4 * q : 4 * q + 4, BOX_SKIP:].rearrange("g r n -> r g n").bitcast(I32),
             )
-        for g in range(0, PAIRS, 2):
+        for r in range(ROUNDS):
+            passes = slice(2 * r, 2 * r + 2)
             nc.sync.dma_start(
-                out=head_codes[:, g : g + 2, BOX_COLS:HEAD_COLS].bitcast(I32),
-                in_=cls_w_words[g : g + 2].rearrange("g p n t -> p g (n t)").bitcast(I32),
+                out=head_codes[:, passes, BOX_COLS:HEAD_COLS].bitcast(I32),
+                in_=cls_w_words[passes].rearrange("g p n t -> p g (n t)").bitcast(I32),
             )
             nc.sync.dma_start(
-                out=head_codes[:, g : g + 2, 0:BOX_COLS].bitcast(I32),
-                in_=bbox_w_words[g : g + 2, :, BOX_SKIP:, :].rearrange("g p n t -> p g (n t)").bitcast(I32),
+                out=head_codes[:, passes, 0:BOX_COLS].bitcast(I32),
+                in_=bbox_w_words[passes, :, BOX_SKIP:, :].rearrange("g p n t -> p g (n t)").bitcast(I32),
             )
-            if FEATURE_LEAD + g < PAIRS:
-                load_features(FEATURE_LEAD + g, 2)
+            if FEATURE_LEAD + r < ROUNDS:
+                load_features(FEATURE_LEAD + r)
 
         make_identity(nc, ident_f32[:])
-        nc.gpsimd.dma_start(out=bias_rows[0:1, HIDDEN + BOX_COLS : HIDDEN + HEAD_COLS], in_=cls_b.rearrange("(o d) -> o d", o=1))
-        nc.gpsimd.dma_start(
-            out=bias_rows[0:1, HIDDEN : HIDDEN + BOX_COLS], in_=bbox_b[BOX_SKIP:].rearrange("(o d) -> o d", o=1)
-        )
+        nc.gpsimd.dma_start(out=bias_rows[0:1, BOX_COLS:HEAD_COLS], in_=cls_b.rearrange("(o d) -> o d", o=1))
+        nc.gpsimd.dma_start(out=bias_rows[0:1, 0:BOX_COLS], in_=bbox_b[BOX_SKIP:].rearrange("(o d) -> o d", o=1))
         nc.gpsimd.dma_start(out=roi_sb[:], in_=roi.rearrange("b i j -> b (i j)"))
-
-        nc.vector.tensor_copy(out=ident_bf16[:], in_=ident_f32[:])
-        nc.scalar.dma_start(out=bias_rows[0:1, 0:HIDDEN], in_=conv_b.rearrange("(o d) -> o d", o=1))
+        for l in range(2):
+            nc.scalar.dma_start(
+                out=conv_bias[LIVE * l : LIVE * (l + 1), :], in_=conv_b.rearrange("(j t) -> j t", t=PACK)
+            )
         nc.scalar.activation(out=table_warm[:], in_=ones[:, 0:1], func=ACT.Exp)
 
         x_words = x_sb[:].bitcast(F32)
@@ -140,172 +142,161 @@ def tile_classifiermodel_kernel(
         x_codes = {}
         x_planes = {}
         h_acc = {}
-        h_sorted = {}
-        h_t = {}
+        h_relu = {}
         h_grouped = {}
 
-        def transpose_features(g):
-            x_t[g] = psum_x.tile([P, 2, 2, P], F32, name="x_t")
+        def transpose_features(r):
             for l in range(2):
-                for u in range(2):
-                    nc.tensor.transpose(
-                        x_t[g][:, l, u, :], x_words[:, 2 * g + l, u : CHANNELS // 2 : 2], ident_f32[:]
-                    )
+                x_t[r, l] = psum_x.tile([P, 2, 2, P], F32, name="x_t")
+                for i in range(2):
+                    for u in range(2):
+                        nc.tensor.transpose(
+                            x_t[r, l][:, i, u, :], x_words[:, 4 * r + 2 * i + l, u : CHANNELS // 2 : 2], ident_f32[:]
+                        )
 
-        def regroup_features(g):
-            x_grouped[g] = work.tile([P, 2, P, PACK], BF16, name="x_grouped", align_bytes=64)
-            nc.scalar.copy(out=x_grouped[g][:].bitcast(F32), in_=x_t[g][:].rearrange("p l u b -> p l b u"))
-
-        def quantise_features(g):
-            x_codes[g] = work.tile([P, 2 * P], U32, name="x_codes", align_bytes=64)
-            x_planes[g] = work.tile([P, 2 * P], U8, name="x_planes", align_bytes=64)
-            nc.vector.quantize_mx(
-                out=x_codes[g][:].bitcast(FP8X4),
-                scales=x_planes[g][:],
-                in_=x_grouped[g][:].rearrange("p l b t -> p (l b t)"),
-            )
-
-        def convolve(g):
-            h_acc[g] = psum_h.tile([P, 2 * HIDDEN], F32, name="h_acc")
+        def regroup_features(r):
             for l in range(2):
-                nc.tensor.matmul_mx(
-                    out=h_acc[g][:, HIDDEN * l : HIDDEN * (l + 1)],
-                    lhsT=x_codes[g][:, P * l : P * (l + 1)].bitcast(FP8X4),
-                    lhsT_scale=x_planes[g][:, P * l : P * (l + 1)],
-                    rhs=conv_codes[:].bitcast(FP8X4),
-                    rhs_scale=conv_plane[:],
-                    start=True,
-                    stop=True,
+                x_grouped[r, l] = work.tile([P, 2, P, PACK], BF16, name="x_grouped", align_bytes=64)
+                nc.scalar.copy(
+                    out=x_grouped[r, l][:].bitcast(F32), in_=x_t[r, l][:].rearrange("p i u b -> p i b u")
                 )
 
-        def add_conv_bias(g):
-            h_sorted[g] = work.tile([P, PACK, P], BF16, name="h_sorted")
-            nc.vector.tensor_tensor(
-                out=h_sorted[g][:],
-                in0=h_acc[g][:].rearrange("b (p t) -> b t p", t=PACK),
-                in1=conv_bias[:],
-                op=ALU.add,
-            )
+        def quantise_features(r):
+            for l in range(2):
+                x_codes[r, l] = work.tile([P, 2 * P], U32, name="x_codes", align_bytes=64)
+                x_planes[r, l] = work.tile([P, 2 * P], U8, name="x_planes", align_bytes=64)
+                nc.vector.quantize_mx(
+                    out=x_codes[r, l][:].bitcast(FP8X4),
+                    scales=x_planes[r, l][:],
+                    in_=x_grouped[r, l][:].rearrange("p i b t -> p (i b t)"),
+                )
 
-        def transpose_hidden(g):
-            h_t[g] = psum_t.tile([P, PACK, P], BF16, name="h_t")
+        def convolve(r):
+            for half in range(2):
+                h_acc[r, half] = psum_h.tile([P, 2, 2 * P], F32, name="h_acc")
+                for k in range(2):
+                    t = 2 * half + k
+                    for l in range(2):
+                        cols = slice(LIVE, 3 * LIVE) if l == 0 else slice(0, 2 * LIVE)
+                        nc.tensor.matmul_mx(
+                            out=h_acc[r, half][:, k, :],
+                            lhsT=padded_codes[:, t, cols].bitcast(FP8X4),
+                            lhsT_scale=padded_plane[:, t, cols],
+                            rhs=x_codes[r, l][:].bitcast(FP8X4),
+                            rhs_scale=x_planes[r, l][:],
+                            start=(l == 0),
+                            stop=(l == 1),
+                        )
+
+        def bias_and_relu(r):
+            h_relu[r] = work.tile([P, PACK, 2 * P], BF16, name="h_relu")
             for t in range(PACK):
-                nc.tensor.transpose(h_t[g][:, t, :], h_sorted[g][:, t, :], ident_bf16[:])
+                nc.scalar.activation(
+                    out=h_relu[r][:, t, :],
+                    in_=h_acc[r, t // 2][:, t % 2, :],
+                    func=ACT.Relu,
+                    bias=conv_bias[:, t : t + 1],
+                )
 
-        def relu_and_regroup(g):
-            h_grouped[g] = work.tile([P, P, PACK], BF16, name="h_grouped", align_bytes=64)
-            nc.scalar.activation(out=h_grouped[g][:], in_=h_t[g][:].rearrange("p t b -> p b t"), func=ACT.Relu)
+        def regroup_hidden(r):
+            for i in range(2):
+                h_grouped[r, i] = work.tile([P, P, PACK], BF16, name="h_grouped", align_bytes=64)
+                nc.vector.tensor_copy(
+                    out=h_grouped[r, i][:], in_=h_relu[r][:, :, P * i : P * (i + 1)].rearrange("p t b -> p b t")
+                )
 
-        def quantise_hidden(g):
-            nc.vector.quantize_mx(
-                out=flat_codes[:, g, :].bitcast(FP8X4),
-                scales=flat_planes[:, g, :],
-                in_=h_grouped[g][:].rearrange("p b t -> p (b t)"),
-            )
+        def quantise_hidden(r):
+            for i in range(2):
+                nc.vector.quantize_mx(
+                    out=flat_codes[:, 2 * r + i, :].bitcast(FP8X4),
+                    scales=flat_planes[:, 2 * r + i, :],
+                    in_=h_grouped[r, i][:].rearrange("p b t -> p (b t)"),
+                )
 
         acc_b1 = psum_acc.tile([P, P], F32)
         acc_wide = psum_acc.tile([P, WIDE], F32)
 
-        def heads(g):
-            for acc, cols in ((acc_b1, slice(0, P)), (acc_wide, slice(P, HEAD_COLS))):
-                nc.tensor.matmul_mx(
-                    out=acc[:],
-                    lhsT=flat_codes[:, g, :].bitcast(FP8X4),
-                    lhsT_scale=flat_planes[:, g, :],
-                    rhs=head_codes[:, g, cols].bitcast(FP8X4),
-                    rhs_scale=head_planes[:, g, cols],
-                    start=(g == 0),
-                    stop=(g == PAIRS - 1),
-                )
+        def heads(r):
+            for g in (2 * r, 2 * r + 1):
+                for acc, cols in ((acc_b1, slice(0, P)), (acc_wide, slice(P, HEAD_COLS))):
+                    nc.tensor.matmul_mx(
+                        out=acc[:],
+                        lhsT=flat_codes[:, g, :].bitcast(FP8X4),
+                        lhsT_scale=flat_planes[:, g, :],
+                        rhs=head_codes[:, g, cols].bitcast(FP8X4),
+                        rhs_scale=head_planes[:, g, cols],
+                        start=(g == 0),
+                        stop=(g == PAIRS - 1),
+                    )
 
-        def spread_conv_bias():
-            spread = psum_h.tile([P, 2 * HIDDEN], F32, name="h_acc")
-            nc.tensor.matmul(out=spread[:, 0:HIDDEN], lhsT=ones[:], rhs=bias_rows[:, 0:HIDDEN], start=True, stop=True)
+        def pad_conv_weights():
             nc.vector.tensor_copy(
-                out=conv_bias[:].rearrange("b t (l j) -> b t l j", l=2),
-                in_=spread[:, 0:HIDDEN]
-                .rearrange("b (j t) -> b t j", t=PACK)
-                .unsqueeze(2)
-                .to_broadcast([P, PACK, 2, HIDDEN // PACK]),
+                out=padded_codes[:, :, LIVE : 2 * LIVE].bitcast(I32),
+                in_=conv_codes[:].bitcast(I32).rearrange("p (j t) -> p t j", t=PACK),
+            )
+            nc.vector.tensor_copy(
+                out=padded_plane[:, :, LIVE : 2 * LIVE].rearrange("p t j -> p j t"),
+                in_=conv_plane[:].rearrange("p (j t) -> p j t", t=PACK),
             )
 
         def spread_head_bias():
-            spread_wide = psum_x.tile([P, WIDE], F32, name="x_t")
-            nc.tensor.matmul(
-                out=spread_wide[:], lhsT=ones[:], rhs=bias_rows[:, HIDDEN : HIDDEN + WIDE], start=True, stop=True
-            )
-            nc.vector.tensor_copy(out=head_bias[:, 0:WIDE], in_=spread_wide[:])
-            spread_rest = psum_x.tile([P, WIDE], F32, name="x_t")
-            nc.tensor.matmul(
-                out=spread_rest[:, 0 : 2 * P],
-                lhsT=ones[:],
-                rhs=bias_rows[:, HIDDEN + WIDE : HIDDEN + WIDE + 2 * P],
-                start=True,
-                stop=True,
-            )
-            nc.vector.tensor_copy(out=head_bias[:, WIDE:HEAD_COLS], in_=spread_rest[:, 0 : HEAD_COLS - WIDE])
+            for cols in (slice(0, WIDE), slice(WIDE, HEAD_COLS)):
+                spread = psum_x.tile([P, WIDE], F32, name="x_t")
+                width = cols.stop - cols.start
+                nc.tensor.matmul(out=spread[:, 0:width], lhsT=ones[:], rhs=bias_rows[:, cols], start=True, stop=True)
+                nc.vector.tensor_copy(out=head_bias[:, cols], in_=spread[:, 0:width])
 
-        def live(g):
-            return 0 <= g < PAIRS
-
-        def pipeline_step(step):
-            if live(step):
+        for step in range(ROUNDS + 2):
+            if step < ROUNDS:
                 transpose_features(step)
-            if live(step - 4):
-                transpose_hidden(step - 4)
-            if live(step):
+            if step == 0:
+                pad_conv_weights()
+            if step < ROUNDS:
                 regroup_features(step)
-            if live(step - 4):
-                relu_and_regroup(step - 4)
-            if live(step - 1):
-                quantise_features(step - 1)
-            if live(step - 5):
-                quantise_hidden(step - 5)
-            if live(step - 2):
-                convolve(step - 2)
-            if live(step - HEAD_LAG):
-                heads(step - HEAD_LAG)
-            if live(step - 2):
-                add_conv_bias(step - 2)
-
-        spread_conv_bias()
-        for step in range(PAIRS):
-            pipeline_step(step)
-        spread_head_bias()
-        for step in range(PAIRS, PAIRS + HEAD_LAG):
-            pipeline_step(step)
+                quantise_features(step)
+            if 1 <= step <= ROUNDS:
+                convolve(step - 1)
+                bias_and_relu(step - 1)
+            if step == 1:
+                spread_head_bias()
+            if step >= 2:
+                heads(step - 2)
+            if 1 <= step <= ROUNDS:
+                regroup_hidden(step - 1)
+                quantise_hidden(step - 1)
 
         planes = keep.tile([P, 5, P], F32)
-        r = keep.tile([P, 4, P], F32)
+        r16 = keep.tile([P, 4, P], F32)
         x_base = keep.tile([P, P], F32)
+        c_bias = keep.tile([P, P], F32)
         nc.gpsimd.tensor_scalar(
-            out=r[:], in0=roi_sb[:].rearrange("b (i j) -> b j i", j=4), scalar1=16.0, scalar2=0.0, op0=ALU.mult, op1=ALU.add
+            out=r16[:], in0=roi_sb[:].rearrange("b (i j) -> b j i", j=4), scalar1=16.0, scalar2=0.0, op0=ALU.mult, op1=ALU.add
         )
-        nc.gpsimd.tensor_scalar(out=planes[:, 1, :], in0=r[:, 1, :], scalar1=1.0, scalar2=0.0, op0=ALU.mult, op1=ALU.add)
-        nc.gpsimd.tensor_tensor(out=x_base[:], in0=head_bias[:, 0:P], in1=r[:, 3, :], op=ALU.mult)
-        nc.gpsimd.tensor_tensor(out=x_base[:], in0=r[:, 0, :], in1=x_base[:], op=ALU.subtract)
+        nc.gpsimd.tensor_scalar(out=planes[:, 1, :], in0=r16[:, 1, :], scalar1=1.0, scalar2=0.0, op0=ALU.mult, op1=ALU.add)
+        nc.gpsimd.tensor_tensor(out=x_base[:], in0=head_bias[:, 0:P], in1=r16[:, 3, :], op=ALU.mult)
+        nc.gpsimd.tensor_tensor(out=x_base[:], in0=r16[:, 0, :], in1=x_base[:], op=ALU.subtract)
+        nc.gpsimd.tensor_tensor(
+            out=c_bias[:], in0=head_bias[:, 3 * P : 4 * P], in1=head_bias[:, 4 * P : 5 * P], op=ALU.subtract
+        )
 
         box = keep.tile([P, 2, P], F32)
-        logits = keep.tile([P, 2, P], F32)
+        c0_shifted = keep.tile([P, P], F32)
         margin = keep.tile([P, P], F32)
         tanh_half = keep.tile([P, P], F32)
         growth = keep.tile([P, 2, P], F32)
         shift = keep.tile([P, P], F32)
         result = keep.tile([P, P, 5], F32)
-        half = WIDE // 2
+        nc.vector.tensor_tensor(out=c0_shifted[:], in0=acc_wide[:, 2 * P : 3 * P], in1=c_bias[:], op=ALU.add)
         nc.vector.tensor_tensor(
-            out=logits[:].rearrange("b j i -> b (j i)"), in0=acc_wide[:, half:WIDE], in1=head_bias[:, P + half : HEAD_COLS], op=ALU.add
+            out=box[:].rearrange("b j i -> b (j i)"), in0=acc_wide[:, 0 : 2 * P], in1=head_bias[:, P : 3 * P], op=ALU.add
         )
-        nc.vector.tensor_tensor(
-            out=box[:].rearrange("b j i -> b (j i)"), in0=acc_wide[:, 0:half], in1=head_bias[:, P : P + half], op=ALU.add
-        )
-        nc.vector.tensor_tensor(out=margin[:], in0=logits[:, 1, :], in1=logits[:, 0, :], op=ALU.subtract)
+        nc.vector.tensor_tensor(out=margin[:], in0=acc_wide[:, 3 * P : 4 * P], in1=c0_shifted[:], op=ALU.subtract)
         nc.scalar.activation(out=tanh_half[:], in_=margin[:], func=ACT.Tanh, scale=0.5)
         nc.vector.tensor_scalar(out=box[:], in0=box[:], scalar1=-10.0, scalar2=10.0, op0=ALU.max, op1=ALU.min)
         nc.scalar.activation(out=growth[:], in_=box[:], func=ACT.Exp)
-        nc.vector.tensor_tensor(out=shift[:], in0=acc_b1[:], in1=r[:, 3, :], op=ALU.mult)
+        nc.vector.tensor_tensor(out=shift[:], in0=acc_b1[:], in1=r16[:, 3, :], op=ALU.mult)
         nc.vector.tensor_tensor(out=planes[:, 0, :], in0=x_base[:], in1=shift[:], op=ALU.subtract)
         nc.vector.tensor_scalar(out=planes[:, 4, :], in0=tanh_half[:], scalar1=0.5, scalar2=0.5, op0=ALU.mult, op1=ALU.add)
-        nc.vector.tensor_tensor(out=planes[:, 2:4, :], in0=r[:, 2:4, :], in1=growth[:], op=ALU.mult)
+        nc.vector.tensor_tensor(out=planes[:, 2:4, :], in0=r16[:, 2:4, :], in1=growth[:], op=ALU.mult)
         nc.vector.tensor_copy(out=result[:], in_=planes[:].rearrange("b j i -> b i j"))
         nc.sync.dma_start(out=out.rearrange("b i j -> b (i j)"), in_=result[:].rearrange("b i j -> b (i j)"))

@@ -21,12 +21,13 @@ LIVE = HIDDEN // PACK
 PAIRS = POSITIONS // 2
 ROUNDS = PAIRS // 2
 CLS_COLS = 256
+HEAD_LAG = 3
 BOX_SKIP = 128
 BOX_COLS = 384
 HEAD_COLS = BOX_COLS + CLS_COLS
 WIDE = 512
 QUADRANTS = 4
-FEATURE_LEAD = 3
+FEATURE_LEAD = 4
 
 FLOPS = 2 * P * POSITIONS * CHANNELS * HIDDEN + 2 * P * POSITIONS * HIDDEN * HEAD_COLS
 BYTES = (
@@ -88,21 +89,27 @@ def tile_classifiermodel_kernel(
 
         x_dram = features.rearrange("b h w c -> b (h w) c")
 
+        def load_positions(r, l):
+            rows = slice(4 * r + l, 4 * r + 4, 2)
+            nc.sync.dma_start(out=x_sb[:, rows, :], in_=x_dram[:, rows, :])
+
         def load_features(r):
             nc.sync.dma_start(out=x_sb[:, 4 * r : 4 * r + 4, :], in_=x_dram[:, 4 * r : 4 * r + 4, :])
 
-        for l in range(2):
-            nc.sync.dma_start(out=x_sb[:, l:4:2, :], in_=x_dram[:, l:4:2, :])
-        nc.sync.dma_start(
-            out=conv_codes[:].bitcast(I32),
-            in_=conv_w_words[0].rearrange("p n t -> p (n t)").bitcast(I32),
-        )
         for q in range(QUADRANTS):
             nc.sync.dma_start(
                 out=conv_plane[32 * q : 32 * q + 4, :].bitcast(I32),
                 in_=conv_w_scales[0, 4 * q : 4 * q + 4, :].bitcast(I32),
             )
-        for r in range(1, FEATURE_LEAD):
+        load_positions(0, 0)
+        load_positions(0, 1)
+        load_positions(1, 0)
+        nc.sync.dma_start(
+            out=conv_codes[:].bitcast(I32),
+            in_=conv_w_words[0].rearrange("p n t -> p (n t)").bitcast(I32),
+        )
+        load_positions(1, 1)
+        for r in range(2, FEATURE_LEAD):
             load_features(r)
         for q in range(QUADRANTS):
             nc.sync.dma_start(
@@ -246,7 +253,7 @@ def tile_classifiermodel_kernel(
                 nc.tensor.matmul(out=spread[:, 0:width], lhsT=ones[:], rhs=bias_rows[:, cols], start=True, stop=True)
                 nc.vector.tensor_copy(out=head_bias[:, cols], in_=spread[:, 0:width])
 
-        for step in range(ROUNDS + 2):
+        for step in range(ROUNDS + HEAD_LAG):
             if step < ROUNDS:
                 transpose_features(step)
             if step == 0:
@@ -259,8 +266,8 @@ def tile_classifiermodel_kernel(
                 bias_and_relu(step - 1)
             if step == 1:
                 spread_head_bias()
-            if step >= 2:
-                heads(step - 2)
+            if step >= HEAD_LAG:
+                heads(step - HEAD_LAG)
             if 1 <= step <= ROUNDS:
                 regroup_hidden(step - 1)
                 quantise_hidden(step - 1)
@@ -286,17 +293,23 @@ def tile_classifiermodel_kernel(
         growth = keep.tile([P, 2, P], F32)
         shift = keep.tile([P, P], F32)
         result = keep.tile([P, P, 5], F32)
-        nc.vector.tensor_tensor(out=c0_shifted[:], in0=acc_wide[:, 2 * P : 3 * P], in1=c_bias[:], op=ALU.add)
         nc.vector.tensor_tensor(
             out=box[:].rearrange("b j i -> b (j i)"), in0=acc_wide[:, 0 : 2 * P], in1=head_bias[:, P : 3 * P], op=ALU.add
         )
-        nc.vector.tensor_tensor(out=margin[:], in0=acc_wide[:, 3 * P : 4 * P], in1=c0_shifted[:], op=ALU.subtract)
-        nc.scalar.activation(out=tanh_half[:], in_=margin[:], func=ACT.Tanh, scale=0.5)
+        nc.vector.tensor_tensor(out=c0_shifted[:], in0=acc_wide[:, 2 * P : 3 * P], in1=c_bias[:], op=ALU.add)
         nc.vector.tensor_scalar(out=box[:], in0=box[:], scalar1=-10.0, scalar2=10.0, op0=ALU.max, op1=ALU.min)
         nc.scalar.activation(out=growth[:], in_=box[:], func=ACT.Exp)
+        nc.vector.tensor_tensor(out=margin[:], in0=acc_wide[:, 3 * P : 4 * P], in1=c0_shifted[:], op=ALU.subtract)
+        nc.scalar.activation(out=tanh_half[:], in_=margin[:], func=ACT.Tanh, scale=0.5)
         nc.vector.tensor_tensor(out=shift[:], in0=acc_b1[:], in1=r16[:, 3, :], op=ALU.mult)
+        nc.scalar.activation(out=planes[:, 4, :], in_=tanh_half[:], func=ACT.Copy, scale=0.5, bias=0.5)
         nc.vector.tensor_tensor(out=planes[:, 0, :], in0=x_base[:], in1=shift[:], op=ALU.subtract)
-        nc.vector.tensor_scalar(out=planes[:, 4, :], in0=tanh_half[:], scalar1=0.5, scalar2=0.5, op0=ALU.mult, op1=ALU.add)
         nc.vector.tensor_tensor(out=planes[:, 2:4, :], in0=r16[:, 2:4, :], in1=growth[:], op=ALU.mult)
-        nc.vector.tensor_copy(out=result[:], in_=planes[:].rearrange("b j i -> b i j"))
-        nc.sync.dma_start(out=out.rearrange("b i j -> b (i j)"), in_=result[:].rearrange("b i j -> b (i j)"))
+        by_proposal = planes[:].rearrange("b j i -> b i j")
+        halves = (slice(0, P // 2), slice(P // 2, P))
+        nc.vector.tensor_copy(out=result[:, halves[0], :], in_=by_proposal[:, halves[0], :])
+        nc.scalar.copy(out=result[:, halves[1], :], in_=by_proposal[:, halves[1], :])
+        for half in halves:
+            nc.sync.dma_start(
+                out=out[:, half, :].rearrange("b i j -> b (i j)"), in_=result[:, half, :].rearrange("b i j -> b (i j)")
+            )

@@ -27,7 +27,7 @@ BOX_COLS = 384
 HEAD_COLS = BOX_COLS + CLS_COLS
 WIDE = 512
 QUADRANTS = 4
-FEATURE_LEAD = 4
+FEATURE_LEAD = 5
 
 FLOPS = 2 * P * POSITIONS * CHANNELS * HIDDEN + 2 * P * POSITIONS * HIDDEN * HEAD_COLS
 BYTES = (
@@ -109,8 +109,6 @@ def tile_classifiermodel_kernel(
             in_=conv_w_words[0].rearrange("p n t -> p (n t)").bitcast(I32),
         )
         load_positions(1, 1)
-        for r in range(2, FEATURE_LEAD):
-            load_features(r)
         for q in range(QUADRANTS):
             nc.sync.dma_start(
                 out=head_planes[32 * q : 32 * q + 4, :, BOX_COLS:HEAD_COLS].bitcast(I32),
@@ -120,6 +118,8 @@ def tile_classifiermodel_kernel(
                 out=head_planes[32 * q : 32 * q + 4, :, 0:BOX_COLS].bitcast(I32),
                 in_=bbox_w_scales[:, 4 * q : 4 * q + 4, BOX_SKIP:].rearrange("g r n -> r g n").bitcast(I32),
             )
+            if 2 + q < FEATURE_LEAD:
+                load_features(2 + q)
         for r in range(ROUNDS):
             passes = slice(2 * r, 2 * r + 2)
             nc.sync.dma_start(

@@ -21,7 +21,7 @@ LIVE = HIDDEN // PACK
 PAIRS = POSITIONS // 2
 ROUNDS = PAIRS // 2
 CLS_COLS = 256
-HEAD_LAG = 3
+HEAD_LAG = 4
 BOX_SKIP = 128
 BOX_COLS = 384
 HEAD_COLS = BOX_COLS + CLS_COLS
@@ -89,10 +89,6 @@ def tile_classifiermodel_kernel(
 
         x_dram = features.rearrange("b h w c -> b (h w) c")
 
-        def load_positions(r, l):
-            rows = slice(4 * r + l, 4 * r + 4, 2)
-            nc.sync.dma_start(out=x_sb[:, rows, :], in_=x_dram[:, rows, :])
-
         def load_features(r):
             nc.sync.dma_start(out=x_sb[:, 4 * r : 4 * r + 4, :], in_=x_dram[:, 4 * r : 4 * r + 4, :])
 
@@ -101,14 +97,13 @@ def tile_classifiermodel_kernel(
                 out=conv_plane[32 * q : 32 * q + 4, :].bitcast(I32),
                 in_=conv_w_scales[0, 4 * q : 4 * q + 4, :].bitcast(I32),
             )
-        load_positions(0, 0)
-        load_positions(0, 1)
-        load_positions(1, 0)
+        for l in range(2):
+            nc.sync.dma_start(out=x_sb[:, l:4:2, :], in_=x_dram[:, l:4:2, :])
         nc.sync.dma_start(
             out=conv_codes[:].bitcast(I32),
             in_=conv_w_words[0].rearrange("p n t -> p (n t)").bitcast(I32),
         )
-        load_positions(1, 1)
+        load_features(1)
         for q in range(QUADRANTS):
             nc.sync.dma_start(
                 out=head_planes[32 * q : 32 * q + 4, :, BOX_COLS:HEAD_COLS].bitcast(I32),
@@ -120,8 +115,9 @@ def tile_classifiermodel_kernel(
             )
             if 2 + q < FEATURE_LEAD:
                 load_features(2 + q)
-        for r in range(ROUNDS):
-            passes = slice(2 * r, 2 * r + 2)
+        nc.sync.dma_start(out=roi_sb[:], in_=roi.rearrange("b i j -> b (i j)"))
+
+        def load_head_words(passes):
             nc.sync.dma_start(
                 out=head_codes[:, passes, BOX_COLS:HEAD_COLS].bitcast(I32),
                 in_=cls_w_words[passes].rearrange("g p n t -> p g (n t)").bitcast(I32),
@@ -130,13 +126,17 @@ def tile_classifiermodel_kernel(
                 out=head_codes[:, passes, 0:BOX_COLS].bitcast(I32),
                 in_=bbox_w_words[passes, :, BOX_SKIP:, :].rearrange("g p n t -> p g (n t)").bitcast(I32),
             )
+
+        for r in range(ROUNDS - 1):
+            load_head_words(slice(2 * r, 2 * r + 2))
             if FEATURE_LEAD + r < ROUNDS:
                 load_features(FEATURE_LEAD + r)
+        for g in (PAIRS - 2, PAIRS - 1):
+            load_head_words(slice(g, g + 1))
 
         make_identity(nc, ident_f32[:])
         nc.gpsimd.dma_start(out=bias_rows[0:1, BOX_COLS:HEAD_COLS], in_=cls_b.rearrange("(o d) -> o d", o=1))
         nc.gpsimd.dma_start(out=bias_rows[0:1, 0:BOX_COLS], in_=bbox_b[BOX_SKIP:].rearrange("(o d) -> o d", o=1))
-        nc.gpsimd.dma_start(out=roi_sb[:], in_=roi.rearrange("b i j -> b (i j)"))
         for l in range(2):
             nc.scalar.dma_start(
                 out=conv_bias[LIVE * l : LIVE * (l + 1), :], in_=conv_b.rearrange("(j t) -> j t", t=PACK)

@@ -21,13 +21,12 @@ LIVE = HIDDEN // PACK
 PAIRS = POSITIONS // 2
 ROUNDS = PAIRS // 2
 CLS_COLS = 256
-HEAD_LAG = 4
+HEAD_LAG = 5
 BOX_SKIP = 128
 BOX_COLS = 384
 HEAD_COLS = BOX_COLS + CLS_COLS
 WIDE = 512
 QUADRANTS = 4
-FEATURE_LEAD = 5
 
 FLOPS = 2 * P * POSITIONS * CHANNELS * HIDDEN + 2 * P * POSITIONS * HIDDEN * HEAD_COLS
 BYTES = (
@@ -89,22 +88,17 @@ def tile_classifiermodel_kernel(
 
         x_dram = features.rearrange("b h w c -> b (h w) c")
 
-        def load_features(r):
-            nc.sync.dma_start(out=x_sb[:, 4 * r : 4 * r + 4, :], in_=x_dram[:, 4 * r : 4 * r + 4, :])
+        def load_features(first_round, n_rounds):
+            rows = slice(4 * first_round, 4 * (first_round + n_rounds))
+            nc.sync.dma_start(out=x_sb[:, rows, :], in_=x_dram[:, rows, :])
 
-        for q in range(QUADRANTS):
+        def load_conv_scales(q):
             nc.sync.dma_start(
                 out=conv_plane[32 * q : 32 * q + 4, :].bitcast(I32),
                 in_=conv_w_scales[0, 4 * q : 4 * q + 4, :].bitcast(I32),
             )
-        for l in range(2):
-            nc.sync.dma_start(out=x_sb[:, l:4:2, :], in_=x_dram[:, l:4:2, :])
-        nc.sync.dma_start(
-            out=conv_codes[:].bitcast(I32),
-            in_=conv_w_words[0].rearrange("p n t -> p (n t)").bitcast(I32),
-        )
-        load_features(1)
-        for q in range(QUADRANTS):
+
+        def load_head_scales(q):
             nc.sync.dma_start(
                 out=head_planes[32 * q : 32 * q + 4, :, BOX_COLS:HEAD_COLS].bitcast(I32),
                 in_=cls_w_scales[:, 4 * q : 4 * q + 4, :].rearrange("g r n -> r g n").bitcast(I32),
@@ -113,9 +107,6 @@ def tile_classifiermodel_kernel(
                 out=head_planes[32 * q : 32 * q + 4, :, 0:BOX_COLS].bitcast(I32),
                 in_=bbox_w_scales[:, 4 * q : 4 * q + 4, BOX_SKIP:].rearrange("g r n -> r g n").bitcast(I32),
             )
-            if 2 + q < FEATURE_LEAD:
-                load_features(2 + q)
-        nc.sync.dma_start(out=roi_sb[:], in_=roi.rearrange("b i j -> b (i j)"))
 
         def load_head_words(passes):
             nc.sync.dma_start(
@@ -127,10 +118,25 @@ def tile_classifiermodel_kernel(
                 in_=bbox_w_words[passes, :, BOX_SKIP:, :].rearrange("g p n t -> p g (n t)").bitcast(I32),
             )
 
+        for l in range(2):
+            nc.sync.dma_start(out=x_sb[:, l:4:2, :], in_=x_dram[:, l:4:2, :])
+        for q in range(QUADRANTS):
+            load_conv_scales(q)
+        nc.sync.dma_start(
+            out=conv_codes[:].bitcast(I32),
+            in_=conv_w_words[0].rearrange("p n t -> p (n t)").bitcast(I32),
+        )
+        load_features(1, 1)
+        load_head_scales(0)
+        load_features(2, 1)
+        load_head_scales(1)
+        load_features(3, 2)
+        load_head_scales(2)
+        load_features(5, 2)
+        load_head_scales(3)
+        nc.sync.dma_start(out=roi_sb[:], in_=roi.rearrange("b i j -> b (i j)"))
         for r in range(ROUNDS - 1):
             load_head_words(slice(2 * r, 2 * r + 2))
-            if FEATURE_LEAD + r < ROUNDS:
-                load_features(FEATURE_LEAD + r)
         for g in (PAIRS - 2, PAIRS - 1):
             load_head_words(slice(g, g + 1))
 

@@ -92,36 +92,41 @@ def tile_classifiermodel_kernel(
             rows = slice(4 * first_round, 4 * (first_round + n_rounds))
             nc.sync.dma_start(out=x_sb[:, rows, :], in_=x_dram[:, rows, :])
 
-        def load_conv_scales(q):
+        def load_conv_scales(k):
             nc.sync.dma_start(
-                out=conv_plane[32 * q : 32 * q + 4, :].bitcast(I32),
-                in_=conv_w_scales[0, 4 * q : 4 * q + 4, :].bitcast(I32),
+                out=conv_plane[k:P:32, :].bitcast(I32), in_=conv_w_scales[0, k : 4 * QUADRANTS : 4, :].bitcast(I32)
             )
 
-        def load_head_scales(q):
+        def load_head_scales(k):
             nc.sync.dma_start(
-                out=head_planes[32 * q : 32 * q + 4, :, BOX_COLS:HEAD_COLS].bitcast(I32),
-                in_=cls_w_scales[:, 4 * q : 4 * q + 4, :].rearrange("g r n -> r g n").bitcast(I32),
+                out=head_planes[k:P:32, :, BOX_COLS:HEAD_COLS].bitcast(I32),
+                in_=cls_w_scales[:, k : 4 * QUADRANTS : 4, :].rearrange("g q n -> q g n").bitcast(I32),
             )
             nc.sync.dma_start(
-                out=head_planes[32 * q : 32 * q + 4, :, 0:BOX_COLS].bitcast(I32),
-                in_=bbox_w_scales[:, 4 * q : 4 * q + 4, BOX_SKIP:].rearrange("g r n -> r g n").bitcast(I32),
+                out=head_planes[k:P:32, :, 0:BOX_COLS].bitcast(I32),
+                in_=bbox_w_scales[:, k : 4 * QUADRANTS : 4, BOX_SKIP:].rearrange("g q n -> q g n").bitcast(I32),
             )
 
-        def load_head_words(passes):
+        def load_cls_words(r):
+            passes = slice(2 * r, 2 * r + 2)
             nc.sync.dma_start(
                 out=head_codes[:, passes, BOX_COLS:HEAD_COLS].bitcast(I32),
                 in_=cls_w_words[passes].rearrange("g p n t -> p g (n t)").bitcast(I32),
             )
+
+        def load_box_words(r, first, last):
+            passes = slice(2 * r, 2 * r + 2)
             nc.sync.dma_start(
-                out=head_codes[:, passes, 0:BOX_COLS].bitcast(I32),
-                in_=bbox_w_words[passes, :, BOX_SKIP:, :].rearrange("g p n t -> p g (n t)").bitcast(I32),
+                out=head_codes[:, passes, first:last].bitcast(I32),
+                in_=bbox_w_words[passes, :, BOX_SKIP + first : BOX_SKIP + last, :]
+                .rearrange("g p n t -> p g (n t)")
+                .bitcast(I32),
             )
 
         for l in range(2):
             nc.sync.dma_start(out=x_sb[:, l:4:2, :], in_=x_dram[:, l:4:2, :])
-        for q in range(QUADRANTS):
-            load_conv_scales(q)
+        for k in range(4):
+            load_conv_scales(k)
         nc.sync.dma_start(
             out=conv_codes[:].bitcast(I32),
             in_=conv_w_words[0].rearrange("p n t -> p (n t)").bitcast(I32),
@@ -136,9 +141,11 @@ def tile_classifiermodel_kernel(
         load_head_scales(3)
         nc.sync.dma_start(out=roi_sb[:], in_=roi.rearrange("b i j -> b (i j)"))
         for r in range(ROUNDS - 1):
-            load_head_words(slice(2 * r, 2 * r + 2))
-        for g in (PAIRS - 2, PAIRS - 1):
-            load_head_words(slice(g, g + 1))
+            load_cls_words(r)
+            load_box_words(r, 0, BOX_COLS)
+        load_cls_words(ROUNDS - 1)
+        load_box_words(ROUNDS - 1, P, BOX_COLS)
+        load_box_words(ROUNDS - 1, 0, P)
 
         make_identity(nc, ident_f32[:])
         nc.gpsimd.dma_start(out=bias_rows[0:1, BOX_COLS:HEAD_COLS], in_=cls_b.rearrange("(o d) -> o d", o=1))
@@ -230,8 +237,8 @@ def tile_classifiermodel_kernel(
         acc_wide = psum_acc.tile([P, WIDE], F32)
 
         def heads(r):
-            for g in (2 * r, 2 * r + 1):
-                for acc, cols in ((acc_b1, slice(0, P)), (acc_wide, slice(P, HEAD_COLS))):
+            for acc, cols in ((acc_wide, slice(P, HEAD_COLS)), (acc_b1, slice(0, P))):
+                for g in (2 * r, 2 * r + 1):
                     nc.tensor.matmul_mx(
                         out=acc[:],
                         lhsT=flat_codes[:, g, :].bitcast(FP8X4),
@@ -307,8 +314,8 @@ def tile_classifiermodel_kernel(
         nc.scalar.activation(out=growth[:], in_=box[:], func=ACT.Exp)
         nc.vector.tensor_tensor(out=margin[:], in0=acc_wide[:, 3 * P : 4 * P], in1=c0_shifted[:], op=ALU.subtract)
         nc.scalar.activation(out=tanh_half[:], in_=margin[:], func=ACT.Tanh, scale=0.5)
-        nc.vector.tensor_tensor(out=shift[:], in0=acc_b1[:], in1=r16[:, 3, :], op=ALU.mult)
         nc.scalar.activation(out=planes[:, 4, :], in_=tanh_half[:], func=ACT.Copy, scale=0.5, bias=0.5)
+        nc.vector.tensor_tensor(out=shift[:], in0=acc_b1[:], in1=r16[:, 3, :], op=ALU.mult)
         nc.vector.tensor_tensor(out=planes[:, 0, :], in0=x_base[:], in1=shift[:], op=ALU.subtract)
         nc.vector.tensor_tensor(out=planes[:, 2:4, :], in0=r16[:, 2:4, :], in1=growth[:], op=ALU.mult)
         by_proposal = planes[:].rearrange("b j i -> b i j")

@@ -26,6 +26,9 @@ BOX_SKIP = 128
 BOX_COLS = 384
 HEAD_COLS = BOX_COLS + CLS_COLS
 WIDE = 512
+ROI_BEHIND = 2
+VECTOR_T = 1
+VECTOR_SHARE = 80
 QUADRANTS = 4
 
 FLOPS = 2 * P * POSITIONS * CHANNELS * HIDDEN + 2 * P * POSITIONS * HIDDEN * HEAD_COLS
@@ -56,7 +59,7 @@ def tile_classifiermodel_kernel(
     nc = tc.nc
     with ExitStack() as stack:
         keep = stack.enter_context(tc.tile_pool(name="keep", bufs=1))
-        work = stack.enter_context(tc.tile_pool(name="work", bufs=3))
+        work = stack.enter_context(tc.tile_pool(name="work", bufs=6))
         psum_x = stack.enter_context(tc.psum_pool(name="psum_x", bufs=4))
         psum_h = stack.enter_context(tc.psum_pool(name="psum_h", bufs=2))
         psum_acc = stack.enter_context(tc.psum_pool(name="psum_acc", bufs=1))
@@ -88,6 +91,10 @@ def tile_classifiermodel_kernel(
 
         x_dram = features.rearrange("b h w c -> b (h w) c")
 
+        def load_positions(r, l):
+            rows = slice(4 * r + l, 4 * r + 4, 2)
+            nc.sync.dma_start(out=x_sb[:, rows, :], in_=x_dram[:, rows, :])
+
         def load_features(first_round, n_rounds):
             rows = slice(4 * first_round, 4 * (first_round + n_rounds))
             nc.sync.dma_start(out=x_sb[:, rows, :], in_=x_dram[:, rows, :])
@@ -107,15 +114,13 @@ def tile_classifiermodel_kernel(
                 in_=bbox_w_scales[:, k : 4 * QUADRANTS : 4, BOX_SKIP:].rearrange("g q n -> q g n").bitcast(I32),
             )
 
-        def load_cls_words(r):
-            passes = slice(2 * r, 2 * r + 2)
+        def load_cls_words(passes):
             nc.sync.dma_start(
                 out=head_codes[:, passes, BOX_COLS:HEAD_COLS].bitcast(I32),
                 in_=cls_w_words[passes].rearrange("g p n t -> p g (n t)").bitcast(I32),
             )
 
-        def load_box_words(r, first, last):
-            passes = slice(2 * r, 2 * r + 2)
+        def load_box_words(passes, first, last):
             nc.sync.dma_start(
                 out=head_codes[:, passes, first:last].bitcast(I32),
                 in_=bbox_w_words[passes, :, BOX_SKIP + first : BOX_SKIP + last, :]
@@ -123,15 +128,16 @@ def tile_classifiermodel_kernel(
                 .bitcast(I32),
             )
 
-        for l in range(2):
-            nc.sync.dma_start(out=x_sb[:, l:4:2, :], in_=x_dram[:, l:4:2, :])
         for k in range(4):
             load_conv_scales(k)
+        load_positions(0, 0)
+        load_positions(0, 1)
+        load_positions(1, 0)
         nc.sync.dma_start(
             out=conv_codes[:].bitcast(I32),
             in_=conv_w_words[0].rearrange("p n t -> p (n t)").bitcast(I32),
         )
-        load_features(1, 1)
+        load_positions(1, 1)
         load_head_scales(0)
         load_features(2, 1)
         load_head_scales(1)
@@ -139,13 +145,17 @@ def tile_classifiermodel_kernel(
         load_head_scales(2)
         load_features(5, 2)
         load_head_scales(3)
-        nc.sync.dma_start(out=roi_sb[:], in_=roi.rearrange("b i j -> b (i j)"))
-        for r in range(ROUNDS - 1):
-            load_cls_words(r)
-            load_box_words(r, 0, BOX_COLS)
-        load_cls_words(ROUNDS - 1)
-        load_box_words(ROUNDS - 1, P, BOX_COLS)
-        load_box_words(ROUNDS - 1, 0, P)
+        for g in range(2):
+            load_cls_words(slice(g, g + 1))
+            load_box_words(slice(g, g + 1), 0, BOX_COLS)
+        for r in range(1, ROUNDS - 1):
+            load_cls_words(slice(2 * r, 2 * r + 2))
+            load_box_words(slice(2 * r, 2 * r + 2), 0, BOX_COLS)
+            if r == ROI_BEHIND:
+                nc.sync.dma_start(out=roi_sb[:], in_=roi.rearrange("b i j -> b (i j)"))
+        load_cls_words(slice(PAIRS - 2, PAIRS))
+        load_box_words(slice(PAIRS - 2, PAIRS), P, BOX_COLS)
+        load_box_words(slice(PAIRS - 2, PAIRS), 0, P)
 
         make_identity(nc, ident_f32[:])
         nc.gpsimd.dma_start(out=bias_rows[0:1, BOX_COLS:HEAD_COLS], in_=cls_b.rearrange("(o d) -> o d", o=1))
@@ -209,14 +219,24 @@ def tile_classifiermodel_kernel(
                         )
 
         def bias_and_relu(r):
-            h_relu[r] = work.tile([P, PACK, 2 * P], BF16, name="h_relu")
+            h_relu[r] = work.tile([P, PACK, 2 * P], BF16, name="h_relu", align_bytes=64)
             for t in range(PACK):
-                nc.scalar.activation(
-                    out=h_relu[r][:, t, :],
-                    in_=h_acc[r, t // 2][:, t % 2, :],
-                    func=ACT.Relu,
-                    bias=conv_bias[:, t : t + 1],
-                )
+                if t == VECTOR_T:
+                    nc.vector.tensor_scalar(
+                        out=h_relu[r][:, t, :],
+                        in0=h_acc[r, t // 2][:, t % 2, :],
+                        scalar1=conv_bias[:, t : t + 1],
+                        scalar2=0.0,
+                        op0=ALU.add,
+                        op1=ALU.max,
+                    )
+                else:
+                    nc.scalar.activation(
+                        out=h_relu[r][:, t, :],
+                        in_=h_acc[r, t // 2][:, t % 2, :],
+                        func=ACT.Relu,
+                        bias=conv_bias[:, t : t + 1],
+                    )
 
         def regroup_hidden(r):
             for i in range(2):
@@ -236,18 +256,22 @@ def tile_classifiermodel_kernel(
         acc_b1 = psum_acc.tile([P, P], F32)
         acc_wide = psum_acc.tile([P, WIDE], F32)
 
+        b1, wide = slice(0, P), slice(P, HEAD_COLS)
+
         def heads(r):
-            for acc, cols in ((acc_wide, slice(P, HEAD_COLS)), (acc_b1, slice(0, P))):
-                for g in (2 * r, 2 * r + 1):
-                    nc.tensor.matmul_mx(
-                        out=acc[:],
-                        lhsT=flat_codes[:, g, :].bitcast(FP8X4),
-                        lhsT_scale=flat_planes[:, g, :],
-                        rhs=head_codes[:, g, cols].bitcast(FP8X4),
-                        rhs_scale=head_planes[:, g, cols],
-                        start=(g == 0),
-                        stop=(g == PAIRS - 1),
-                    )
+            passes = [(g, acc, cols) for g in (2 * r, 2 * r + 1) for acc, cols in ((acc_b1, b1), (acc_wide, wide))]
+            if r == ROUNDS - 1:
+                passes = passes[1::2] + passes[0::2]
+            for g, acc, cols in passes:
+                nc.tensor.matmul_mx(
+                    out=acc[:],
+                    lhsT=flat_codes[:, g, :].bitcast(FP8X4),
+                    lhsT_scale=flat_planes[:, g, :],
+                    rhs=head_codes[:, g, cols].bitcast(FP8X4),
+                    rhs_scale=head_planes[:, g, cols],
+                    start=(g == 0),
+                    stop=(g == PAIRS - 1),
+                )
 
         def pad_conv_weights():
             nc.vector.tensor_copy(
@@ -319,10 +343,10 @@ def tile_classifiermodel_kernel(
         nc.vector.tensor_tensor(out=planes[:, 0, :], in0=x_base[:], in1=shift[:], op=ALU.subtract)
         nc.vector.tensor_tensor(out=planes[:, 2:4, :], in0=r16[:, 2:4, :], in1=growth[:], op=ALU.mult)
         by_proposal = planes[:].rearrange("b j i -> b i j")
-        halves = (slice(0, P // 2), slice(P // 2, P))
-        nc.vector.tensor_copy(out=result[:, halves[0], :], in_=by_proposal[:, halves[0], :])
-        nc.scalar.copy(out=result[:, halves[1], :], in_=by_proposal[:, halves[1], :])
-        for half in halves:
+        shares = (slice(0, VECTOR_SHARE), slice(VECTOR_SHARE, P))
+        nc.vector.tensor_copy(out=result[:, shares[0], :], in_=by_proposal[:, shares[0], :])
+        nc.scalar.copy(out=result[:, shares[1], :], in_=by_proposal[:, shares[1], :])
+        for share in shares:
             nc.sync.dma_start(
-                out=out[:, half, :].rearrange("b i j -> b (i j)"), in_=result[:, half, :].rearrange("b i j -> b (i j)")
+                out=out[:, share, :].rearrange("b i j -> b (i j)"), in_=result[:, share, :].rearrange("b i j -> b (i j)")
             )

from contextlib import ExitStack

import concourse.mybir as mybir
from concourse.masks import make_identity

F32 = mybir.dt.float32
BF16 = mybir.dt.bfloat16
I32 = mybir.dt.int32
U32 = mybir.dt.uint32
U8 = mybir.dt.uint8
FP8X4 = mybir.dt.float8_e4m3fn_x4
ALU = mybir.AluOpType
ACT = mybir.ActivationFunctionType

P = 128
PACK = 4
POSITIONS = 28
CHANNELS = 512
HIDDEN = 256
LIVE = HIDDEN // PACK
PAIRS = POSITIONS // 2
ROUNDS = PAIRS // 2
CLS_COLS = 256
HEAD_LAG = 5
BOX_SKIP = 128
BOX_COLS = 384
HEAD_COLS = BOX_COLS + CLS_COLS
WIDE = 512
ROI_BEHIND = 2
VECTOR_T = 1
VECTOR_SHARE = 80
QUADRANTS = 4

FLOPS = 2 * P * POSITIONS * CHANNELS * HIDDEN + 2 * P * POSITIONS * HIDDEN * HEAD_COLS
BYTES = (
    2 * P * POSITIONS * CHANNELS
    + 2 * P * P * 4
    + CHANNELS * HIDDEN + CHANNELS * HIDDEN // 32 + 2 * HIDDEN
    + POSITIONS * HIDDEN * HEAD_COLS + POSITIONS * HIDDEN * HEAD_COLS // 32 + 2 * HEAD_COLS
    + 4 * P * P * 5
)


def tile_classifiermodel_kernel(
    tc,
    features,
    roi,
    conv_w_words,
    conv_w_scales,
    conv_b,
    cls_w_words,
    cls_w_scales,
    cls_b,
    bbox_w_words,
    bbox_w_scales,
    bbox_b,
    out,
):
    nc = tc.nc
    with ExitStack() as stack:
        keep = stack.enter_context(tc.tile_pool(name="keep", bufs=1))
        work = stack.enter_context(tc.tile_pool(name="work", bufs=6))
        psum_x = stack.enter_context(tc.psum_pool(name="psum_x", bufs=4))
        psum_h = stack.enter_context(tc.psum_pool(name="psum_h", bufs=2))
        psum_acc = stack.enter_context(tc.psum_pool(name="psum_acc", bufs=1))
        stack.enter_context(tc.manual_schedule())

        x_sb = keep.tile([P, POSITIONS, CHANNELS], BF16)
        conv_codes = keep.tile([P, HIDDEN], U32, align_bytes=64)
        conv_plane = keep.tile([P, HIDDEN], U8, align_bytes=64)
        padded_codes = keep.tile([P, PACK, 3 * LIVE], U32, align_bytes=64)
        padded_plane = keep.tile([P, PACK, 3 * LIVE], U8, align_bytes=64)
        head_codes = keep.tile([P, PAIRS, HEAD_COLS], U32, align_bytes=64)
        head_planes = keep.tile([P, PAIRS, HEAD_COLS], U8, align_bytes=64)
        flat_codes = keep.tile([P, PAIRS, P], U32, align_bytes=64)
        flat_planes = keep.tile([P, PAIRS, P], U8, align_bytes=64)
        roi_sb = keep.tile([P, P * 4], BF16)
        bias_rows = keep.tile([P, HEAD_COLS], BF16)
        conv_bias = keep.tile([P, PACK], BF16)
        ones = keep.tile([P, P], BF16)
        ident_f32 = keep.tile([P, P], F32)
        head_bias = keep.tile([P, HEAD_COLS], F32)
        table_warm = keep.tile([P, 1], F32)

        nc.vector.memset(conv_plane[:].bitcast(I32), 0)
        nc.vector.memset(bias_rows[:], 0.0)
        nc.vector.memset(ones[:], 1.0)
        nc.vector.memset(padded_codes[:].rearrange("p t n -> p (t n)").bitcast(I32), 0)
        nc.vector.memset(padded_plane[:].rearrange("p t n -> p (t n)").bitcast(I32), 0)
        nc.vector.memset(head_planes[:].rearrange("p g n -> p (g n)").bitcast(I32), 0)

        x_dram = features.rearrange("b h w c -> b (h w) c")

        def load_positions(r, l):
            rows = slice(4 * r + l, 4 * r + 4, 2)
            nc.sync.dma_start(out=x_sb[:, rows, :], in_=x_dram[:, rows, :])

        def load_features(first_round, n_rounds):
            rows = slice(4 * first_round, 4 * (first_round + n_rounds))
            nc.sync.dma_start(out=x_sb[:, rows, :], in_=x_dram[:, rows, :])

        def load_conv_scales(k):
            nc.sync.dma_start(
                out=conv_plane[k:P:32, :].bitcast(I32), in_=conv_w_scales[0, k : 4 * QUADRANTS : 4, :].bitcast(I32)
            )

        def load_head_scales(k):
            nc.sync.dma_start(
                out=head_planes[k:P:32, :, BOX_COLS:HEAD_COLS].bitcast(I32),
                in_=cls_w_scales[:, k : 4 * QUADRANTS : 4, :].rearrange("g q n -> q g n").bitcast(I32),
            )
            nc.sync.dma_start(
                out=head_planes[k:P:32, :, 0:BOX_COLS].bitcast(I32),
                in_=bbox_w_scales[:, k : 4 * QUADRANTS : 4, BOX_SKIP:].rearrange("g q n -> q g n").bitcast(I32),
            )

        def load_cls_words(passes):
            nc.sync.dma_start(
                out=head_codes[:, passes, BOX_COLS:HEAD_COLS].bitcast(I32),
                in_=cls_w_words[passes].rearrange("g p n t -> p g (n t)").bitcast(I32),
            )

        def load_box_words(passes, first, last):
            nc.sync.dma_start(
                out=head_codes[:, passes, first:last].bitcast(I32),
                in_=bbox_w_words[passes, :, BOX_SKIP + first : BOX_SKIP + last, :]
                .rearrange("g p n t -> p g (n t)")
                .bitcast(I32),
            )

        for k in range(4):
            load_conv_scales(k)
        load_positions(0, 0)
        load_positions(0, 1)
        load_positions(1, 0)
        nc.sync.dma_start(
            out=conv_codes[:].bitcast(I32),
            in_=conv_w_words[0].rearrange("p n t -> p (n t)").bitcast(I32),
        )
        load_positions(1, 1)
        load_head_scales(0)
        load_features(2, 1)
        load_head_scales(1)
        load_features(3, 2)
        load_head_scales(2)
        load_features(5, 2)
        load_head_scales(3)
        for g in range(2):
            load_cls_words(slice(g, g + 1))
            load_box_words(slice(g, g + 1), 0, BOX_COLS)
        for r in range(1, ROUNDS - 1):
            load_cls_words(slice(2 * r, 2 * r + 2))
            load_box_words(slice(2 * r, 2 * r + 2), 0, BOX_COLS)
            if r == ROI_BEHIND:
                nc.sync.dma_start(out=roi_sb[:], in_=roi.rearrange("b i j -> b (i j)"))
        load_cls_words(slice(PAIRS - 2, PAIRS))
        load_box_words(slice(PAIRS - 2, PAIRS), P, BOX_COLS)
        load_box_words(slice(PAIRS - 2, PAIRS), 0, P)

        make_identity(nc, ident_f32[:])
        nc.gpsimd.dma_start(out=bias_rows[0:1, BOX_COLS:HEAD_COLS], in_=cls_b.rearrange("(o d) -> o d", o=1))
        nc.gpsimd.dma_start(out=bias_rows[0:1, 0:BOX_COLS], in_=bbox_b[BOX_SKIP:].rearrange("(o d) -> o d", o=1))
        for l in range(2):
            nc.scalar.dma_start(
                out=conv_bias[LIVE * l : LIVE * (l + 1), :], in_=conv_b.rearrange("(j t) -> j t", t=PACK)
            )
        nc.scalar.activation(out=table_warm[:], in_=ones[:, 0:1], func=ACT.Exp)

        x_words = x_sb[:].bitcast(F32)
        x_t = {}
        x_grouped = {}
        x_codes = {}
        x_planes = {}
        h_acc = {}
        h_relu = {}
        h_grouped = {}

        def transpose_features(r):
            for l in range(2):
                x_t[r, l] = psum_x.tile([P, 2, 2, P], F32, name="x_t")
                for i in range(2):
                    for u in range(2):
                        nc.tensor.transpose(
                            x_t[r, l][:, i, u, :], x_words[:, 4 * r + 2 * i + l, u : CHANNELS // 2 : 2], ident_f32[:]
                        )

        def regroup_features(r):
            for l in range(2):
                x_grouped[r, l] = work.tile([P, 2, P, PACK], BF16, name="x_grouped", align_bytes=64)
                nc.scalar.copy(
                    out=x_grouped[r, l][:].bitcast(F32), in_=x_t[r, l][:].rearrange("p i u b -> p i b u")
                )

        def quantise_features(r):
            for l in range(2):
                x_codes[r, l] = work.tile([P, 2 * P], U32, name="x_codes", align_bytes=64)
                x_planes[r, l] = work.tile([P, 2 * P], U8, name="x_planes", align_bytes=64)
                nc.vector.quantize_mx(
                    out=x_codes[r, l][:].bitcast(FP8X4),
                    scales=x_planes[r, l][:],
                    in_=x_grouped[r, l][:].rearrange("p i b t -> p (i b t)"),
                )

        def convolve(r):
            for half in range(2):
                h_acc[r, half] = psum_h.tile([P, 2, 2 * P], F32, name="h_acc")
                for k in range(2):
                    t = 2 * half + k
                    for l in range(2):
                        cols = slice(LIVE, 3 * LIVE) if l == 0 else slice(0, 2 * LIVE)
                        nc.tensor.matmul_mx(
                            out=h_acc[r, half][:, k, :],
                            lhsT=padded_codes[:, t, cols].bitcast(FP8X4),
                            lhsT_scale=padded_plane[:, t, cols],
                            rhs=x_codes[r, l][:].bitcast(FP8X4),
                            rhs_scale=x_planes[r, l][:],
                            start=(l == 0),
                            stop=(l == 1),
                        )

        def bias_and_relu(r):
            h_relu[r] = work.tile([P, PACK, 2 * P], BF16, name="h_relu", align_bytes=64)
            for t in range(PACK):
                if t == VECTOR_T:
                    nc.vector.tensor_scalar(
                        out=h_relu[r][:, t, :],
                        in0=h_acc[r, t // 2][:, t % 2, :],
                        scalar1=conv_bias[:, t : t + 1],
                        scalar2=0.0,
                        op0=ALU.add,
                        op1=ALU.max,
                    )
                else:
                    nc.scalar.activation(
                        out=h_relu[r][:, t, :],
                        in_=h_acc[r, t // 2][:, t % 2, :],
                        func=ACT.Relu,
                        bias=conv_bias[:, t : t + 1],
                    )

        def regroup_hidden(r):
            for i in range(2):
                h_grouped[r, i] = work.tile([P, P, PACK], BF16, name="h_grouped", align_bytes=64)
                nc.vector.tensor_copy(
                    out=h_grouped[r, i][:], in_=h_relu[r][:, :, P * i : P * (i + 1)].rearrange("p t b -> p b t")
                )

        def quantise_hidden(r):
            for i in range(2):
                nc.vector.quantize_mx(
                    out=flat_codes[:, 2 * r + i, :].bitcast(FP8X4),
                    scales=flat_planes[:, 2 * r + i, :],
                    in_=h_grouped[r, i][:].rearrange("p b t -> p (b t)"),
                )

        acc_b1 = psum_acc.tile([P, P], F32)
        acc_wide = psum_acc.tile([P, WIDE], F32)

        b1, wide = slice(0, P), slice(P, HEAD_COLS)

        def heads(r):
            passes = [(g, acc, cols) for g in (2 * r, 2 * r + 1) for acc, cols in ((acc_b1, b1), (acc_wide, wide))]
            if r == ROUNDS - 1:
                passes = passes[1::2] + passes[0::2]
            for g, acc, cols in passes:
                nc.tensor.matmul_mx(
                    out=acc[:],
                    lhsT=flat_codes[:, g, :].bitcast(FP8X4),
                    lhsT_scale=flat_planes[:, g, :],
                    rhs=head_codes[:, g, cols].bitcast(FP8X4),
                    rhs_scale=head_planes[:, g, cols],
                    start=(g == 0),
                    stop=(g == PAIRS - 1),
                )

        def pad_conv_weights():
            nc.vector.tensor_copy(
                out=padded_codes[:, :, LIVE : 2 * LIVE].bitcast(I32),
                in_=conv_codes[:].bitcast(I32).rearrange("p (j t) -> p t j", t=PACK),
            )
            nc.vector.tensor_copy(
                out=padded_plane[:, :, LIVE : 2 * LIVE].rearrange("p t j -> p j t"),
                in_=conv_plane[:].rearrange("p (j t) -> p j t", t=PACK),
            )

        def spread_head_bias():
            for cols in (slice(0, WIDE), slice(WIDE, HEAD_COLS)):
                spread = psum_x.tile([P, WIDE], F32, name="x_t")
                width = cols.stop - cols.start
                nc.tensor.matmul(out=spread[:, 0:width], lhsT=ones[:], rhs=bias_rows[:, cols], start=True, stop=True)
                nc.vector.tensor_copy(out=head_bias[:, cols], in_=spread[:, 0:width])

        for step in range(ROUNDS + HEAD_LAG):
            if step < ROUNDS:
                transpose_features(step)
            if step == 0:
                pad_conv_weights()
            if step < ROUNDS:
                regroup_features(step)
                quantise_features(step)
            if 1 <= step <= ROUNDS:
                convolve(step - 1)
                bias_and_relu(step - 1)
            if step == 1:
                spread_head_bias()
            if step >= HEAD_LAG:
                heads(step - HEAD_LAG)
            if 1 <= step <= ROUNDS:
                regroup_hidden(step - 1)
                quantise_hidden(step - 1)

        planes = keep.tile([P, 5, P], F32)
        r16 = keep.tile([P, 4, P], F32)
        x_base = keep.tile([P, P], F32)
        c_bias = keep.tile([P, P], F32)
        nc.gpsimd.tensor_scalar(
            out=r16[:], in0=roi_sb[:].rearrange("b (i j) -> b j i", j=4), scalar1=16.0, scalar2=0.0, op0=ALU.mult, op1=ALU.add
        )
        nc.gpsimd.tensor_scalar(out=planes[:, 1, :], in0=r16[:, 1, :], scalar1=1.0, scalar2=0.0, op0=ALU.mult, op1=ALU.add)
        nc.gpsimd.tensor_tensor(out=x_base[:], in0=head_bias[:, 0:P], in1=r16[:, 3, :], op=ALU.mult)
        nc.gpsimd.tensor_tensor(out=x_base[:], in0=r16[:, 0, :], in1=x_base[:], op=ALU.subtract)
        nc.gpsimd.tensor_tensor(
            out=c_bias[:], in0=head_bias[:, 3 * P : 4 * P], in1=head_bias[:, 4 * P : 5 * P], op=ALU.subtract
        )

        box = keep.tile([P, 2, P], F32)
        c0_shifted = keep.tile([P, P], F32)
        margin = keep.tile([P, P], F32)
        tanh_half = keep.tile([P, P], F32)
        growth = keep.tile([P, 2, P], F32)
        shift = keep.tile([P, P], F32)
        result = keep.tile([P, P, 5], F32)
        nc.vector.tensor_tensor(
            out=box[:].rearrange("b j i -> b (j i)"), in0=acc_wide[:, 0 : 2 * P], in1=head_bias[:, P : 3 * P], op=ALU.add
        )
        nc.vector.tensor_tensor(out=c0_shifted[:], in0=acc_wide[:, 2 * P : 3 * P], in1=c_bias[:], op=ALU.add)
        nc.vector.tensor_scalar(out=box[:], in0=box[:], scalar1=-10.0, scalar2=10.0, op0=ALU.max, op1=ALU.min)
        nc.scalar.activation(out=growth[:], in_=box[:], func=ACT.Exp)
        nc.vector.tensor_tensor(out=margin[:], in0=acc_wide[:, 3 * P : 4 * P], in1=c0_shifted[:], op=ALU.subtract)
        nc.scalar.activation(out=tanh_half[:], in_=margin[:], func=ACT.Tanh, scale=0.5)
        nc.scalar.activation(out=planes[:, 4, :], in_=tanh_half[:], func=ACT.Copy, scale=0.5, bias=0.5)
        nc.vector.tensor_tensor(out=shift[:], in0=acc_b1[:], in1=r16[:, 3, :], op=ALU.mult)
        nc.vector.tensor_tensor(out=planes[:, 0, :], in0=x_base[:], in1=shift[:], op=ALU.subtract)
        nc.vector.tensor_tensor(out=planes[:, 2:4, :], in0=r16[:, 2:4, :], in1=growth[:], op=ALU.mult)
        by_proposal = planes[:].rearrange("b j i -> b i j")
        shares = (slice(0, VECTOR_SHARE), slice(VECTOR_SHARE, P))
        nc.vector.tensor_copy(out=result[:, shares[0], :], in_=by_proposal[:, shares[0], :])
        nc.scalar.copy(out=result[:, shares[1], :], in_=by_proposal[:, shares[1], :])
        for share in shares:
            nc.sync.dma_start(
                out=out[:, share, :].rearrange("b i j -> b (i j)"), in_=result[:, share, :].rearrange("b i j -> b (i j)")
            )
